import numpy as np
import ml_dtypes


def mxq(x, axis, fmt="e4m3"):
    dtype, down = {"e4m3": (ml_dtypes.float8_e4m3fn, 7), "e5m2": (ml_dtypes.float8_e5m2, 14)}[fmt]
    v = np.moveaxis(np.asarray(x, np.float32).astype(ml_dtypes.bfloat16).astype(np.float64), axis, -1)
    blocks = v.reshape(v.shape[:-1] + (-1, 32))
    amax = np.abs(blocks).max(-1, keepdims=True)
    byte = np.maximum(np.where(amax > 0, np.frexp(amax)[1] - 1 + 127, 0) - down, 1)
    scale = np.exp2(byte - 127.0)
    codes = (blocks / scale).astype(np.float32).astype(dtype).astype(np.float64)
    return np.moveaxis((codes * scale).reshape(v.shape), -1, axis)


WIDE = False


def mx_kscale(k):
    if not WIDE:
        return np.ones(k)
    levels = np.array([10, -10, 5, -5, 0])
    a = np.random.permutation(np.resize(levels, k // 512 * 4)).reshape(k // 512, 4)
    idx = np.arange(k)
    return np.exp2(a[idx // 512, idx % 128 // 32])


BF16 = ml_dtypes.bfloat16


def bf(x):
    return np.asarray(x, np.float32).astype(BF16)


def f64(x):
    return np.asarray(x).astype(np.float64)


E2M1 = np.array([0.0, 0.5, 1.0, 1.5, 2.0, 3.0, 4.0, 6.0, -0.0, -0.5, -1.0, -1.5, -2.0, -3.0, -4.0, -6.0])


def pack_weight(w, fmt):
    k, n = w.shape
    w = f64(bf(w)).reshape(k // 32, 32, n)
    amax = np.abs(w).max(1)
    if fmt == "e4m3":
        byte = np.frexp(amax)[1] - 1 + 127 - 7
    else:
        mant, ex = np.frexp(amax / 6.0)
        byte = np.where(mant > 0.5, ex, ex - 1) + 127
    byte = np.clip(np.where(amax > 0, byte, 1), 1, 254)
    scaled = (w * np.exp2(127.0 - byte)[:, None, :]).reshape(k, n).astype(np.float32)
    by_word = np.ascontiguousarray(scaled.reshape(k // 512, 128, 4, n).transpose(0, 1, 3, 2))
    if fmt == "e4m3":
        words = by_word.astype(ml_dtypes.float8_e4m3fn).view(np.uint8)
    else:
        c = by_word.astype(ml_dtypes.float4_e2m1fn).view(np.uint8) & 0xF
        words = c[..., 0::2] | (c[..., 1::2] << 4)
    return np.ascontiguousarray(words), np.ascontiguousarray(byte.astype(np.uint8).reshape(k // 512, 16, n))


def unpack_weight(words, scales, fmt):
    g, p, n, _ = words.shape
    if fmt == "e4m3":
        vals = np.ascontiguousarray(words).view(ml_dtypes.float8_e4m3fn).astype(np.float64)
    else:
        nib = np.empty((g, p, n, 4), np.uint8)
        nib[..., 0::2] = words & 0xF
        nib[..., 1::2] = words >> 4
        vals = E2M1[nib]
    vals = vals * np.repeat(np.exp2(scales.astype(np.float64) - 127.0), 8, axis=1)[..., None]
    return vals.transpose(0, 1, 3, 2).reshape(g * 512, n)

def pack4(w):
    words, scales = pack_weight(w, "e2m1")
    return words.reshape(words.shape[0], 128, -1), scales


def unpack4(words, scales):
    return unpack_weight(words.reshape(words.shape[0], 128, -1, 2), scales, "e2m1")


B, NF, GH, GW, DX, DIM, NH, CHUNK, SINK, MAXF = 1, 8, 16, 16, 1024, 1024, 8, 2, 1, 4
L = NF * GH * GW
HD = DIM // NH
C = HD // 2
DS = C // 3
DT = C - 2 * DS
MT = max(NF, GH, GW)
EPS = 1e-6


def rope_tables():
    def tab(d):
        inv = 1.0 / (10000.0 ** (np.arange(d) / d))
        ang = np.outer(np.arange(MT), inv)
        return np.cos(ang), np.sin(ang)
    ct, st = tab(DT)
    ch, sh = tab(DS)
    cw, sw = tab(DS)
    return np.concatenate([ct, ch, cw], axis=1), np.concatenate([st, sh, sw], axis=1)


def pos_table(tab):
    t = np.broadcast_to(tab[:NF, :DT][:, None, None, :], (NF, GH, GW, DT))
    hh = np.broadcast_to(tab[:GH, DT:DT + DS][None, :, None, :], (NF, GH, GW, DS))
    ww = np.broadcast_to(tab[:GW, DT + DS:][None, None, :, :], (NF, GH, GW, DS))
    return np.concatenate([t, hh, ww], axis=-1).reshape(L, C)


def setup_inputs():
    s = mx_kscale(DX)
    fc, fs = rope_tables()
    x = bf(np.random.standard_normal((B, L, DX)) * s)
    w = np.random.standard_normal((DIM, DX)) / np.sqrt(DX) / s[None, :]
    W_words, W_scales = pack4(np.ascontiguousarray(w.T))
    b = bf(np.random.standard_normal(DIM) * 0.3)
    g = bf(1.0 + 0.1 * np.random.standard_normal(DIM))
    return {"x": x,
            "W_words": W_words, "W_scales": W_scales,
            "b": b,
            "g": g,
            "freqs_cos": bf(fc), "freqs_sin": bf(fs)}


def reference(x, W_words, W_scales, b, g, freqs_cos, freqs_sin):
    y = (mxq(f64(x), 2, "e4m3") @ unpack4(W_words, W_scales)) + f64(b)
    z = y * (1.0 / np.sqrt(np.mean(y * y, axis=-1, keepdims=True) + EPS)) * f64(g)
    co = pos_table(f64(freqs_cos))[None, :, None, :]
    si = pos_table(f64(freqs_sin))[None, :, None, :]
    a = z.reshape(B, L, NH, C, 2)
    xr, xi = a[..., 0], a[..., 1]
    return np.stack([xr * co - xi * si, xr * si + xi * co], axis=-1).reshape(B, L, NH, HD)

@@ -1,0 +1,314 @@
+from contextlib import ExitStack
+
+import concourse.mybir as mybir
+from concourse.masks import make_identity
+
+F32 = mybir.dt.float32
+BF16 = mybir.dt.bfloat16
+I32 = mybir.dt.int32
+U32 = mybir.dt.uint32
+U8 = mybir.dt.uint8
+FP8X4 = mybir.dt.float8_e4m3fn_x4
+FP4X4 = mybir.dt.float4_e2m1fn_x4
+ALU = mybir.AluOpType
+ACT = mybir.ActivationFunctionType
+
+P = 128
+TOKENS = 2048
+K = 1024
+FEATURES = 1024
+HEADS = 8
+HEAD = 128
+K_PASS = 512
+PASSES = K // K_PASS
+BLOCK = 512
+TILES = TOKENS // P
+BLOCK_TILES = BLOCK // P
+BLOCKS = TOKENS // BLOCK
+FRAMES = 8
+FRAME_PAIRS = 22
+GRID_PAIRS = 21
+TABLE_PAIRS = 64
+F_COLS = 2 * FRAME_PAIRS
+RC_COLS = HEAD - F_COLS
+BANK = 512
+BANK_HEADS = BANK // HEAD
+EPS = 1e-6
+
+FLOPS = 2 * TOKENS * K * FEATURES
+
+
+def tile_causalwanselfattention_pa_kernel(
+    tc, x, W_words, W_scales, b, g, freqs_cos, freqs_sin, out
+):
+    nc = tc.nc
+    x_rows = x.rearrange("o l k -> (o l) k")
+    out_rows = out.rearrange("o l h d -> (o l) (h d)")
+
+    with ExitStack() as ctx:
+        const = ctx.enter_context(tc.tile_pool(name="const", bufs=1))
+        quant = ctx.enter_context(tc.tile_pool(name="quant", bufs=2))
+        feat = ctx.enter_context(tc.tile_pool(name="feat", bufs=2 * HEADS))
+        work = ctx.enter_context(tc.tile_pool(name="work", bufs=3))
+        small = ctx.enter_context(tc.tile_pool(name="small", bufs=4))
+        psum_x = ctx.enter_context(tc.psum_pool(name="psum_x", bufs=2))
+        psum_a = ctx.enter_context(tc.psum_pool(name="psum_a", bufs=2))
+        psum_y = ctx.enter_context(tc.psum_pool(name="psum_y", bufs=2))
+
+        g_all = const.tile([P, FEATURES], BF16, name="g_all")
+        nc.scalar.dma_start(out=g_all[:], in_=g.partition_broadcast(P))
+        b_rows = const.tile([P, P], BF16, name="b_rows")
+        nc.vector.memset(b_rows[:], 0.0)
+        nc.scalar.dma_start(out=b_rows[0:HEADS, :], in_=b.rearrange("(h d) -> h d", d=HEAD))
+        by_frame = {}
+        by_row = {}
+        by_col = {}
+        for name, table in (("cos", freqs_cos), ("sin", freqs_sin)):
+            by_frame[name] = const.tile([P, FRAMES * TABLE_PAIRS], BF16, name=name + "_frame")
+            nc.scalar.dma_start(
+                out=by_frame[name][:],
+                in_=table[0:FRAMES, :].rearrange("f j -> (f j)").partition_broadcast(P),
+            )
+            by_col[name] = const.tile([P, TABLE_PAIRS], BF16, name=name + "_col")
+            nc.scalar.dma_start(
+                out=by_col[name][:], in_=table.unsqueeze(0).to_broadcast([8, 16, TABLE_PAIRS])
+            )
+            for half in range(2):
+                by_row[name, half] = const.tile(
+                    [P, TABLE_PAIRS], BF16, name="%s_row%d" % (name, half)
+                )
+                nc.scalar.dma_start(
+                    out=by_row[name, half][:],
+                    in_=table[8 * half : 8 * half + 8, :]
+                    .unsqueeze(1)
+                    .to_broadcast([8, 16, TABLE_PAIRS]),
+                )
+
+        x_blocks = [const.tile([P, BLOCK_TILES, K], BF16, name="x%d" % blk) for blk in range(BLOCKS)]
+        for tt in range(BLOCK_TILES):
+            nc.sync.dma_start(out=x_blocks[0][:, tt, :], in_=x_rows[tt * P : (tt + 1) * P, :])
+
+        w_words = const.tile([P, PASSES, 2 * FEATURES], U8, name="w_words", align_bytes=64)
+        nc.sync.dma_start(
+            out=w_words[:].bitcast(I32), in_=W_words.rearrange("c p n -> p c n").bitcast(I32)
+        )
+        w_scales = const.tile([P, PASSES, FEATURES], U8, name="w_scales", align_bytes=64)
+        nc.vector.memset(w_scales[:].bitcast(I32), 0)
+        scale_rows = W_scales.rearrange("c (q r) n -> r q c n", r=4)
+        for r in range(4):
+            nc.sync.dma_start(
+                out=w_scales[r:P:32, :, :].bitcast(I32), in_=scale_rows[r].bitcast(I32)
+            )
+        for blk in range(1, BLOCKS):
+            nc.sync.dma_start(
+                out=x_blocks[blk][:],
+                in_=x_rows[blk * BLOCK : (blk + 1) * BLOCK, :].rearrange("(t p) k -> p t k", p=P),
+            )
+
+        ident = const.tile([P, P], F32, name="ident")
+        make_identity(nc, ident[:])
+        eps_col = const.tile([P, 1], F32, name="eps_col")
+        nc.vector.memset(eps_col[:], EPS)
+        warm = const.tile([P, 1], F32, name="warm")
+        nc.scalar.activation(out=warm[:], in_=eps_col[:], func=ACT.Abs_reciprocal_sqrt)
+
+        b_rows32 = const.tile([P, P], F32, name="b_rows32")
+        nc.vector.tensor_copy(out=b_rows32[:], in_=b_rows[:])
+        b_ps = psum_x.tile([P, PASSES, 2, P], F32, name="b_ps", tag="xt")
+        nc.tensor.transpose(b_ps[:, 0, 0, :], b_rows32[:], ident[:])
+        b_col = const.tile([P, HEADS], F32, name="b_col")
+        nc.vector.tensor_copy(out=b_col[:], in_=b_ps[:, 0, 0, 0:HEADS])
+
+        sign = const.tile([P, 2], F32, name="sign")
+        nc.vector.memset(sign[:, 0:1], 1.0)
+        nc.vector.memset(sign[:, 1:2], -1.0)
+        g_signed = const.tile([P, FEATURES], F32, name="g_signed")
+        nc.vector.tensor_tensor(
+            out=g_signed[:].rearrange("p (j i) -> p j i", i=2),
+            in0=g_all[:].rearrange("p (j i) -> p j i", i=2),
+            in1=sign[:].unsqueeze(1).to_broadcast([P, FEATURES // 2, 2]),
+            op=ALU.mult,
+        )
+        gain = {
+            "cos": g_all[:].rearrange("p (h d) -> p h d", d=HEAD),
+            "sin": g_signed[:].rearrange("p (h d) -> p h d", d=HEAD),
+        }
+
+        def fill_table(engine, dst, gain_cols, angles, pairs):
+            engine.tensor_tensor(
+                out=dst.rearrange("p h (j i) -> p h j i", i=2),
+                in0=gain_cols.rearrange("p h (j i) -> p h j i", i=2),
+                in1=angles.unsqueeze(1).unsqueeze(3).to_broadcast([P, HEADS, pairs, 2]),
+                op=ALU.mult,
+            )
+
+        tab_rc = {}
+        tab_f = {}
+        for name in ("cos", "sin"):
+            tab_rc[name] = const.tile([P, 2, HEADS, RC_COLS], F32, name=name + "_tab_rc")
+            tab_f[name] = const.tile([P, FRAMES, HEADS, F_COLS], F32, name=name + "_tab_f")
+        row_end = FRAME_PAIRS + GRID_PAIRS
+
+        def fill_grid_tables(half):
+            for name in ("cos", "sin"):
+                fill_table(
+                    nc.vector,
+                    tab_rc[name][:, half, :, 0 : 2 * GRID_PAIRS],
+                    gain[name][:, :, F_COLS : 2 * row_end],
+                    by_row[name, half][:, FRAME_PAIRS:row_end],
+                    GRID_PAIRS,
+                )
+                fill_table(
+                    nc.vector,
+                    tab_rc[name][:, half, :, 2 * GRID_PAIRS : RC_COLS],
+                    gain[name][:, :, 2 * row_end : HEAD],
+                    by_col[name][:, row_end:TABLE_PAIRS],
+                    GRID_PAIRS,
+                )
+
+        def fill_frame_tables(engine, f):
+            for name in ("cos", "sin"):
+                fill_table(
+                    engine,
+                    tab_f[name][:, f, :, :],
+                    gain[name][:, :, 0:F_COLS],
+                    by_frame[name][:, f * TABLE_PAIRS : f * TABLE_PAIRS + FRAME_PAIRS],
+                    FRAME_PAIRS,
+                )
+
+        grouped = {}
+        codes = {}
+        planes = {}
+        y_feat = {}
+
+        def transpose_x(t):
+            blk, tt = divmod(t, BLOCK_TILES)
+            if tt == 0:
+                grouped[blk] = quant.tile([P, PASSES, 4 * BLOCK], BF16, name="grouped", align_bytes=64)
+            x_words = x_blocks[blk][:, tt, :].bitcast(F32)
+            xt = psum_x.tile([P, PASSES, 2, P], F32, name="xt")
+            for c in range(PASSES):
+                for u in range(2):
+                    nc.tensor.transpose(
+                        xt[:, c, u, :], x_words[:, 256 * c + u : 256 * (c + 1) : 2], ident[:]
+                    )
+            dst = grouped[blk][:].bitcast(F32).rearrange("p c (r u) -> p c r u", u=2)
+            if t % 2 == 0:
+                nc.scalar.copy(
+                    out=dst[:, :, tt * P : (tt + 1) * P, :], in_=xt[:].rearrange("p c u r -> p c r u")
+                )
+            else:
+                nc.vector.tensor_copy(
+                    out=dst[:, :, tt * P : (tt + 1) * P, :], in_=xt[:].rearrange("p c u r -> p c r u")
+                )
+
+        def quantise_x(blk):
+            codes[blk] = quant.tile([P, PASSES, BLOCK], U32, name="codes", align_bytes=64)
+            planes[blk] = quant.tile([P, PASSES, BLOCK], U8, name="planes", align_bytes=64)
+            for c in range(PASSES):
+                nc.vector.quantize_mx(
+                    out=codes[blk][:, c, :].bitcast(FP8X4),
+                    scales=planes[blk][:, c, :],
+                    in_=grouped[blk][:, c, :],
+                )
+
+        def project(blk, h):
+            acc = psum_a.tile([P, BLOCK], F32, name="acc")
+            for c in range(PASSES):
+                nc.tensor.matmul_mx(
+                    out=acc[:],
+                    lhsT=w_words[:, c, 2 * HEAD * h : 2 * HEAD * (h + 1)].bitcast(FP4X4),
+                    lhsT_scale=w_scales[:, c, HEAD * h : HEAD * (h + 1)],
+                    rhs=codes[blk][:, c, :].bitcast(FP8X4),
+                    rhs_scale=planes[blk][:, c, :],
+                    start=(c == 0),
+                    stop=(c == PASSES - 1),
+                )
+            y_feat[blk, h] = feat.tile([P, BLOCK], F32, name="y_feat")
+            nc.scalar.activation(
+                out=y_feat[blk, h][:], in_=acc[:], func=ACT.Identity, bias=b_col[:, h : h + 1], scale=1.0
+            )
+
+        def finish(t):
+            blk, tt = divmod(t, BLOCK_TILES)
+            frame, half = divmod(t, 2)
+            y_ps = [psum_y.tile([P, BANK], F32, name="y_ps%d" % k) for k in range(2)]
+            for h in range(HEADS):
+                k, hk = divmod(h, BANK_HEADS)
+                nc.tensor.transpose(
+                    y_ps[k][:, hk * HEAD : (hk + 1) * HEAD],
+                    y_feat[blk, h][:, tt * P : (tt + 1) * P],
+                    ident[:],
+                )
+            sums = small.tile([P, 2], F32, name="sums")
+            for k in range(2):
+                squares = work.tile([P, BANK], F32, name="squares%d" % k)
+                nc.scalar.activation(
+                    out=squares[:], in_=y_ps[k][:], func=ACT.Square, accum_out=sums[:, k : k + 1]
+                )
+            part = small.tile([P, 1], F32, name="part")
+            nc.scalar.activation(
+                out=part[:], in_=sums[:, 1:2], func=ACT.Identity, bias=eps_col[:, 0:1], scale=1.0 / FEATURES
+            )
+            inv = small.tile([P, 1], F32, name="inv")
+            nc.scalar.activation(
+                out=inv[:], in_=sums[:, 0:1], func=ACT.Abs_reciprocal_sqrt, bias=part[:, 0:1], scale=1.0 / FEATURES
+            )
+
+            prod = {}
+            for name in ("cos", "sin"):
+                prod[name] = work.tile([P, FEATURES], F32, name=name + "_prod")
+            for k in range(2):
+                heads = slice(k * BANK_HEADS, (k + 1) * BANK_HEADS)
+                src = y_ps[k][:].rearrange("p (h d) -> p h d", d=HEAD)
+                for name in ("cos", "sin"):
+                    dst = prod[name][:].rearrange("p (h d) -> p h d", d=HEAD)
+                    nc.vector.scalar_tensor_tensor(
+                        out=dst[:, heads, 0:F_COLS],
+                        in0=src[:, :, 0:F_COLS],
+                        scalar=inv[:, 0:1],
+                        in1=tab_f[name][:, frame, heads, :],
+                        op0=ALU.mult,
+                        op1=ALU.mult,
+                    )
+                    nc.vector.scalar_tensor_tensor(
+                        out=dst[:, heads, F_COLS:HEAD],
+                        in0=src[:, :, F_COLS:HEAD],
+                        scalar=inv[:, 0:1],
+                        in1=tab_rc[name][:, half, heads, :],
+                        op0=ALU.mult,
+                        op1=ALU.mult,
+                    )
+            rotated = work.tile([P, FEATURES], F32, name="rotated")
+            nc.gpsimd.tensor_tensor(
+                out=rotated[:].rearrange("p (j i) -> p j i", i=2),
+                in0=prod["cos"][:].rearrange("p (j i) -> p j i", i=2),
+                in1=prod["sin"][:].rearrange("p (j i) -> p j i", i=2)[:, :, ::-1],
+                op=ALU.add,
+            )
+            nc.sync.dma_start(out=out_rows[t * P : (t + 1) * P, :], in_=rotated[:])
+
+        for t in range(BLOCK_TILES):
+            transpose_x(t)
+        quantise_x(0)
+        fill_grid_tables(0)
+        fill_frame_tables(nc.vector, 0)
+        fill_grid_tables(1)
+        for f in range(1, FRAMES // 2):
+            fill_frame_tables(nc.vector, f)
+        for f in range(FRAMES // 2, FRAMES):
+            fill_frame_tables(nc.gpsimd, f)
+        for h in range(HEADS):
+            project(0, h)
+        for blk in range(BLOCKS):
+            for tt in range(BLOCK_TILES):
+                finish(blk * BLOCK_TILES + tt)
+                if blk + 1 < BLOCKS:
+                    if tt < 2:
+                        transpose_x((blk + 1) * BLOCK_TILES + 2 * tt)
+                        transpose_x((blk + 1) * BLOCK_TILES + 2 * tt + 1)
+                        if tt == 1:
+                            quantise_x(blk + 1)
+                    else:
+                        for h in range(4 * (tt - 2), 4 * (tt - 1)):
+                            project(blk + 1, h)

@@ -21,10 +21,7 @@ HEADS = 8
 HEAD = 128
 K_PASS = 512
 PASSES = K // K_PASS
-BLOCK = 512
 TILES = TOKENS // P
-BLOCK_TILES = BLOCK // P
-BLOCKS = TOKENS // BLOCK
 FRAMES = 8
 FRAME_PAIRS = 22
 GRID_PAIRS = 21
@@ -33,7 +30,10 @@ F_COLS = 2 * FRAME_PAIRS
 RC_COLS = HEAD - F_COLS
 BANK = 512
 BANK_HEADS = BANK // HEAD
+BANKS = FEATURES // BANK
 EPS = 1e-6
+X_LEAD = 3
+MX_LEAD = 1
 
 FLOPS = 2 * TOKENS * K * FEATURES
 
@@ -47,47 +47,31 @@ def tile_causalwanselfattention_pa_kernel(
 
     with ExitStack() as ctx:
         const = ctx.enter_context(tc.tile_pool(name="const", bufs=1))
-        quant = ctx.enter_context(tc.tile_pool(name="quant", bufs=2))
-        feat = ctx.enter_context(tc.tile_pool(name="feat", bufs=2 * HEADS))
+        quant = ctx.enter_context(tc.tile_pool(name="quant", bufs=3))
+        feat = ctx.enter_context(tc.tile_pool(name="feat", bufs=2))
         work = ctx.enter_context(tc.tile_pool(name="work", bufs=3))
         small = ctx.enter_context(tc.tile_pool(name="small", bufs=4))
         psum_x = ctx.enter_context(tc.psum_pool(name="psum_x", bufs=2))
-        psum_a = ctx.enter_context(tc.psum_pool(name="psum_a", bufs=2))
+        psum_a = ctx.enter_context(tc.psum_pool(name="psum_a", bufs=1))
         psum_y = ctx.enter_context(tc.psum_pool(name="psum_y", bufs=2))
+        ctx.enter_context(tc.manual_schedule())
+        x_tiles = [const.tile([P, K], BF16, name="x%d" % t) for t in range(TILES)]
 
-        g_all = const.tile([P, FEATURES], BF16, name="g_all")
-        nc.scalar.dma_start(out=g_all[:], in_=g.partition_broadcast(P))
+        def load_x(t):
+            nc.sync.dma_start(out=x_tiles[t][:], in_=x_rows[t * P : (t + 1) * P, :])
+
+        def load_angles(rows, kind):
+            pair = {}
+            for name, table in (("cos", freqs_cos), ("sin", freqs_sin)):
+                src = rows(table)
+                pair[name] = const.tile([P, src.shape[-1]], BF16, name="%s_%s" % (name, kind))
+                nc.sync.dma_start(out=pair[name][:], in_=src)
+            return pair
+
+        load_x(0)
         b_rows = const.tile([P, P], BF16, name="b_rows")
         nc.vector.memset(b_rows[:], 0.0)
-        nc.scalar.dma_start(out=b_rows[0:HEADS, :], in_=b.rearrange("(h d) -> h d", d=HEAD))
-        by_frame = {}
-        by_row = {}
-        by_col = {}
-        for name, table in (("cos", freqs_cos), ("sin", freqs_sin)):
-            by_frame[name] = const.tile([P, FRAMES * TABLE_PAIRS], BF16, name=name + "_frame")
-            nc.scalar.dma_start(
-                out=by_frame[name][:],
-                in_=table[0:FRAMES, :].rearrange("f j -> (f j)").partition_broadcast(P),
-            )
-            by_col[name] = const.tile([P, TABLE_PAIRS], BF16, name=name + "_col")
-            nc.scalar.dma_start(
-                out=by_col[name][:], in_=table.unsqueeze(0).to_broadcast([8, 16, TABLE_PAIRS])
-            )
-            for half in range(2):
-                by_row[name, half] = const.tile(
-                    [P, TABLE_PAIRS], BF16, name="%s_row%d" % (name, half)
-                )
-                nc.scalar.dma_start(
-                    out=by_row[name, half][:],
-                    in_=table[8 * half : 8 * half + 8, :]
-                    .unsqueeze(1)
-                    .to_broadcast([8, 16, TABLE_PAIRS]),
-                )
-
-        x_blocks = [const.tile([P, BLOCK_TILES, K], BF16, name="x%d" % blk) for blk in range(BLOCKS)]
-        for tt in range(BLOCK_TILES):
-            nc.sync.dma_start(out=x_blocks[0][:, tt, :], in_=x_rows[tt * P : (tt + 1) * P, :])
-
+        nc.sync.dma_start(out=b_rows[0:HEADS, :], in_=b.rearrange("(h d) -> h d", d=HEAD))
         w_words = const.tile([P, PASSES, 2 * FEATURES], U8, name="w_words", align_bytes=64)
         nc.sync.dma_start(
             out=w_words[:].bitcast(I32), in_=W_words.rearrange("c p n -> p c n").bitcast(I32)
@@ -99,11 +83,24 @@ def tile_causalwanselfattention_pa_kernel(
             nc.sync.dma_start(
                 out=w_scales[r:P:32, :, :].bitcast(I32), in_=scale_rows[r].bitcast(I32)
             )
-        for blk in range(1, BLOCKS):
-            nc.sync.dma_start(
-                out=x_blocks[blk][:],
-                in_=x_rows[blk * BLOCK : (blk + 1) * BLOCK, :].rearrange("(t p) k -> p t k", p=P),
-            )
+        g_all = const.tile([P, FEATURES], BF16, name="g_all")
+        nc.sync.dma_start(out=g_all[:], in_=g.partition_broadcast(P))
+        load_x(1)
+        by_col = load_angles(lambda tab: tab.unsqueeze(0).to_broadcast([8, 16, TABLE_PAIRS]), "col")
+        by_row = {}
+        by_row[0] = load_angles(
+            lambda tab: tab[0:8, :].unsqueeze(1).to_broadcast([8, 16, TABLE_PAIRS]), "row0"
+        )
+        by_frame = load_angles(
+            lambda tab: tab[0:FRAMES, :].rearrange("f j -> (f j)").partition_broadcast(P), "frame"
+        )
+        load_x(2)
+        load_x(3)
+        by_row[1] = load_angles(
+            lambda tab: tab[8:16, :].unsqueeze(1).to_broadcast([8, 16, TABLE_PAIRS]), "row1"
+        )
+        for t in range(4, TILES):
+            load_x(t)
 
         ident = const.tile([P, P], F32, name="ident")
         make_identity(nc, ident[:])
@@ -120,10 +117,10 @@ def tile_causalwanselfattention_pa_kernel(
         nc.vector.tensor_copy(out=b_col[:], in_=b_ps[:, 0, 0, 0:HEADS])
 
         sign = const.tile([P, 2], F32, name="sign")
-        nc.vector.memset(sign[:, 0:1], 1.0)
-        nc.vector.memset(sign[:, 1:2], -1.0)
+        nc.gpsimd.memset(sign[:, 0:1], 1.0)
+        nc.gpsimd.memset(sign[:, 1:2], -1.0)
         g_signed = const.tile([P, FEATURES], F32, name="g_signed")
-        nc.vector.tensor_tensor(
+        nc.gpsimd.tensor_tensor(
             out=g_signed[:].rearrange("p (j i) -> p j i", i=2),
             in0=g_all[:].rearrange("p (j i) -> p j i", i=2),
             in1=sign[:].unsqueeze(1).to_broadcast([P, FEATURES // 2, 2]),
@@ -133,6 +130,12 @@ def tile_causalwanselfattention_pa_kernel(
             "cos": g_all[:].rearrange("p (h d) -> p h d", d=HEAD),
             "sin": g_signed[:].rearrange("p (h d) -> p h d", d=HEAD),
         }
+        tab_rc = {}
+        tab_f = {}
+        for name in ("cos", "sin"):
+            tab_rc[name] = const.tile([P, 2, HEADS, RC_COLS], F32, name=name + "_tab_rc")
+            tab_f[name] = const.tile([P, FRAMES, HEADS, F_COLS], F32, name=name + "_tab_f")
+        row_end = FRAME_PAIRS + GRID_PAIRS
 
         def fill_table(engine, dst, gain_cols, angles, pairs):
             engine.tensor_tensor(
@@ -142,20 +145,13 @@ def tile_causalwanselfattention_pa_kernel(
                 op=ALU.mult,
             )
 
-        tab_rc = {}
-        tab_f = {}
-        for name in ("cos", "sin"):
-            tab_rc[name] = const.tile([P, 2, HEADS, RC_COLS], F32, name=name + "_tab_rc")
-            tab_f[name] = const.tile([P, FRAMES, HEADS, F_COLS], F32, name=name + "_tab_f")
-        row_end = FRAME_PAIRS + GRID_PAIRS
-
         def fill_grid_tables(half):
             for name in ("cos", "sin"):
                 fill_table(
                     nc.vector,
                     tab_rc[name][:, half, :, 0 : 2 * GRID_PAIRS],
                     gain[name][:, :, F_COLS : 2 * row_end],
-                    by_row[name, half][:, FRAME_PAIRS:row_end],
+                    by_row[half][name][:, FRAME_PAIRS:row_end],
                     GRID_PAIRS,
                 )
                 fill_table(
@@ -166,10 +162,10 @@ def tile_causalwanselfattention_pa_kernel(
                     GRID_PAIRS,
                 )
 
-        def fill_frame_tables(engine, f):
+        for f in range(FRAMES):
             for name in ("cos", "sin"):
                 fill_table(
-                    engine,
+                    nc.gpsimd,
                     tab_f[name][:, f, :, :],
                     gain[name][:, :, 0:F_COLS],
                     by_frame[name][:, f * TABLE_PAIRS : f * TABLE_PAIRS + FRAME_PAIRS],
@@ -182,67 +178,60 @@ def tile_causalwanselfattention_pa_kernel(
         y_feat = {}
 
         def transpose_x(t):
-            blk, tt = divmod(t, BLOCK_TILES)
-            if tt == 0:
-                grouped[blk] = quant.tile([P, PASSES, 4 * BLOCK], BF16, name="grouped", align_bytes=64)
-            x_words = x_blocks[blk][:, tt, :].bitcast(F32)
+            x_words = x_tiles[t][:].bitcast(F32)
             xt = psum_x.tile([P, PASSES, 2, P], F32, name="xt")
             for c in range(PASSES):
                 for u in range(2):
                     nc.tensor.transpose(
                         xt[:, c, u, :], x_words[:, 256 * c + u : 256 * (c + 1) : 2], ident[:]
                     )
-            dst = grouped[blk][:].bitcast(F32).rearrange("p c (r u) -> p c r u", u=2)
-            if t % 2 == 0:
-                nc.scalar.copy(
-                    out=dst[:, :, tt * P : (tt + 1) * P, :], in_=xt[:].rearrange("p c u r -> p c r u")
-                )
-            else:
-                nc.vector.tensor_copy(
-                    out=dst[:, :, tt * P : (tt + 1) * P, :], in_=xt[:].rearrange("p c u r -> p c r u")
-                )
-
-        def quantise_x(blk):
-            codes[blk] = quant.tile([P, PASSES, BLOCK], U32, name="codes", align_bytes=64)
-            planes[blk] = quant.tile([P, PASSES, BLOCK], U8, name="planes", align_bytes=64)
-            for c in range(PASSES):
-                nc.vector.quantize_mx(
-                    out=codes[blk][:, c, :].bitcast(FP8X4),
-                    scales=planes[blk][:, c, :],
-                    in_=grouped[blk][:, c, :],
-                )
-
-        def project(blk, h):
-            acc = psum_a.tile([P, BLOCK], F32, name="acc")
-            for c in range(PASSES):
-                nc.tensor.matmul_mx(
-                    out=acc[:],
-                    lhsT=w_words[:, c, 2 * HEAD * h : 2 * HEAD * (h + 1)].bitcast(FP4X4),
-                    lhsT_scale=w_scales[:, c, HEAD * h : HEAD * (h + 1)],
-                    rhs=codes[blk][:, c, :].bitcast(FP8X4),
-                    rhs_scale=planes[blk][:, c, :],
-                    start=(c == 0),
-                    stop=(c == PASSES - 1),
-                )
-            y_feat[blk, h] = feat.tile([P, BLOCK], F32, name="y_feat")
-            nc.scalar.activation(
-                out=y_feat[blk, h][:], in_=acc[:], func=ACT.Identity, bias=b_col[:, h : h + 1], scale=1.0
+            grouped[t] = quant.tile([P, PASSES * 4 * P], BF16, name="grouped", align_bytes=64)
+            nc.vector.tensor_copy(
+                out=grouped[t][:].bitcast(F32).rearrange("p (c r u) -> p c r u", c=PASSES, u=2),
+                in_=xt[:].rearrange("p c u r -> p c r u"),
             )
 
-        def finish(t):
-            blk, tt = divmod(t, BLOCK_TILES)
+        def quantise_x(t):
+            codes[t] = quant.tile([P, PASSES, P], U32, name="codes", align_bytes=64)
+            planes[t] = quant.tile([P, PASSES, P], U8, name="planes", align_bytes=64)
+            nc.vector.quantize_mx(
+                out=codes[t][:].rearrange("p c r -> p (c r)").bitcast(FP8X4),
+                scales=planes[t][:].rearrange("p c r -> p (c r)"),
+                in_=grouped[t][:],
+            )
+
+        def project(t):
+            acc = [psum_a.tile([P, BANK_HEADS, P], F32, name="acc%d" % k) for k in range(BANKS)]
+            y_feat[t] = feat.tile([P, HEADS, P], F32, name="y_feat")
+            for k in range(BANKS):
+                for hk in range(BANK_HEADS):
+                    h = k * BANK_HEADS + hk
+                    for c in range(PASSES):
+                        nc.tensor.matmul_mx(
+                            out=acc[k][:, hk, :],
+                            lhsT=w_words[:, c, 2 * HEAD * h : 2 * HEAD * (h + 1)].bitcast(FP4X4),
+                            lhsT_scale=w_scales[:, c, HEAD * h : HEAD * (h + 1)],
+                            rhs=codes[t][:, c, :].bitcast(FP8X4),
+                            rhs_scale=planes[t][:, c, :],
+                            start=(c == 0),
+                            stop=(c == PASSES - 1),
+                        )
+                for hk in range(BANK_HEADS):
+                    h = k * BANK_HEADS + hk
+                    nc.scalar.activation(
+                        out=y_feat[t][:, h, :], in_=acc[k][:, hk, :], func=ACT.Identity,
+                        bias=b_col[:, h : h + 1], scale=1.0,
+                    )
+
+        def finish(t, between_banks):
             frame, half = divmod(t, 2)
-            y_ps = [psum_y.tile([P, BANK], F32, name="y_ps%d" % k) for k in range(2)]
+            y_ps = [psum_y.tile([P, BANK_HEADS, HEAD], F32, name="y_ps%d" % k) for k in range(BANKS)]
             for h in range(HEADS):
                 k, hk = divmod(h, BANK_HEADS)
-                nc.tensor.transpose(
-                    y_ps[k][:, hk * HEAD : (hk + 1) * HEAD],
-                    y_feat[blk, h][:, tt * P : (tt + 1) * P],
-                    ident[:],
-                )
-            sums = small.tile([P, 2], F32, name="sums")
-            for k in range(2):
-                squares = work.tile([P, BANK], F32, name="squares%d" % k)
+                nc.tensor.transpose(y_ps[k][:, hk, :], y_feat[t][:, h, :], ident[:])
+            sums = small.tile([P, BANKS], F32, name="sums")
+            for k in range(BANKS):
+                squares = work.tile([P, BANK_HEADS, HEAD], F32, name="squares%d" % k)
                 nc.scalar.activation(
                     out=squares[:], in_=y_ps[k][:], func=ACT.Square, accum_out=sums[:, k : k + 1]
                 )
@@ -252,63 +241,56 @@ def tile_causalwanselfattention_pa_kernel(
             )
             inv = small.tile([P, 1], F32, name="inv")
             nc.scalar.activation(
-                out=inv[:], in_=sums[:, 0:1], func=ACT.Abs_reciprocal_sqrt, bias=part[:, 0:1], scale=1.0 / FEATURES
+                out=inv[:], in_=sums[:, 0:1], func=ACT.Abs_reciprocal_sqrt, bias=part[:, 0:1],
+                scale=1.0 / FEATURES,
             )
-
             prod = {}
             for name in ("cos", "sin"):
-                prod[name] = work.tile([P, FEATURES], F32, name=name + "_prod")
-            for k in range(2):
+                prod[name] = work.tile([P, HEADS, HEAD], F32, name=name + "_prod")
+            for k in range(BANKS):
                 heads = slice(k * BANK_HEADS, (k + 1) * BANK_HEADS)
-                src = y_ps[k][:].rearrange("p (h d) -> p h d", d=HEAD)
                 for name in ("cos", "sin"):
-                    dst = prod[name][:].rearrange("p (h d) -> p h d", d=HEAD)
                     nc.vector.scalar_tensor_tensor(
-                        out=dst[:, heads, 0:F_COLS],
-                        in0=src[:, :, 0:F_COLS],
+                        out=prod[name][:, heads, 0:F_COLS],
+                        in0=y_ps[k][:, :, 0:F_COLS],
                         scalar=inv[:, 0:1],
                         in1=tab_f[name][:, frame, heads, :],
                         op0=ALU.mult,
                         op1=ALU.mult,
                     )
                     nc.vector.scalar_tensor_tensor(
-                        out=dst[:, heads, F_COLS:HEAD],
-                        in0=src[:, :, F_COLS:HEAD],
+                        out=prod[name][:, heads, F_COLS:HEAD],
+                        in0=y_ps[k][:, :, F_COLS:HEAD],
                         scalar=inv[:, 0:1],
                         in1=tab_rc[name][:, half, heads, :],
                         op0=ALU.mult,
                         op1=ALU.mult,
                     )
+                if k == 0:
+                    between_banks()
             rotated = work.tile([P, FEATURES], F32, name="rotated")
             nc.gpsimd.tensor_tensor(
                 out=rotated[:].rearrange("p (j i) -> p j i", i=2),
-                in0=prod["cos"][:].rearrange("p (j i) -> p j i", i=2),
-                in1=prod["sin"][:].rearrange("p (j i) -> p j i", i=2)[:, :, ::-1],
+                in0=prod["cos"][:].rearrange("p h (j i) -> p (h j) i", i=2),
+                in1=prod["sin"][:].rearrange("p h (j i) -> p (h j) i", i=2)[:, :, ::-1],
                 op=ALU.add,
             )
             nc.sync.dma_start(out=out_rows[t * P : (t + 1) * P, :], in_=rotated[:])
 
-        for t in range(BLOCK_TILES):
-            transpose_x(t)
-        quantise_x(0)
-        fill_grid_tables(0)
-        fill_frame_tables(nc.vector, 0)
-        fill_grid_tables(1)
-        for f in range(1, FRAMES // 2):
-            fill_frame_tables(nc.vector, f)
-        for f in range(FRAMES // 2, FRAMES):
-            fill_frame_tables(nc.gpsimd, f)
-        for h in range(HEADS):
-            project(0, h)
-        for blk in range(BLOCKS):
-            for tt in range(BLOCK_TILES):
-                finish(blk * BLOCK_TILES + tt)
-                if blk + 1 < BLOCKS:
-                    if tt < 2:
-                        transpose_x((blk + 1) * BLOCK_TILES + 2 * tt)
-                        transpose_x((blk + 1) * BLOCK_TILES + 2 * tt + 1)
-                        if tt == 1:
-                            quantise_x(blk + 1)
-                    else:
-                        for h in range(4 * (tt - 2), 4 * (tt - 1)):
-                            project(blk + 1, h)
+        for step in range(-X_LEAD, TILES):
+            ahead = step + X_LEAD
+
+            def quantise_ahead():
+                if ahead < TILES:
+                    quantise_x(ahead)
+
+            if ahead < TILES:
+                transpose_x(ahead)
+            if 0 <= step + MX_LEAD < TILES:
+                project(step + MX_LEAD)
+            if step >= 0:
+                finish(step, quantise_ahead)
+            else:
+                quantise_ahead()
+            if step + 1 in (0, 1):
+                fill_grid_tables(step + 1)

@@ -269,7 +269,7 @@ def tile_causalwanselfattention_pa_kernel(
                 if k == 0:
                     between_banks()
             rotated = work.tile([P, FEATURES], F32, name="rotated")
-            nc.gpsimd.tensor_tensor(
+            nc.vector.tensor_tensor(
                 out=rotated[:].rearrange("p (j i) -> p j i", i=2),
                 in0=prod["cos"][:].rearrange("p h (j i) -> p (h j) i", i=2),
                 in1=prod["sin"][:].rearrange("p h (j i) -> p (h j) i", i=2)[:, :, ::-1],

@@ -186,7 +186,7 @@ def tile_causalwanselfattention_pa_kernel(
                         xt[:, c, u, :], x_words[:, 256 * c + u : 256 * (c + 1) : 2], ident[:]
                     )
             grouped[t] = quant.tile([P, PASSES * 4 * P], BF16, name="grouped", align_bytes=64)
-            nc.vector.tensor_copy(
+            nc.scalar.copy(
                 out=grouped[t][:].bitcast(F32).rearrange("p (c r u) -> p c r u", c=PASSES, u=2),
                 in_=xt[:].rearrange("p c u r -> p c r u"),
             )
@@ -269,7 +269,7 @@ def tile_causalwanselfattention_pa_kernel(
                 if k == 0:
                     between_banks()
             rotated = work.tile([P, FEATURES], F32, name="rotated")
-            nc.vector.tensor_tensor(
+            nc.gpsimd.tensor_tensor(
                 out=rotated[:].rearrange("p (j i) -> p j i", i=2),
                 in0=prod["cos"][:].rearrange("p h (j i) -> p (h j) i", i=2),
                 in1=prod["sin"][:].rearrange("p h (j i) -> p (h j) i", i=2)[:, :, ::-1],

@@ -34,6 +34,8 @@ BANKS = FEATURES // BANK
 EPS = 1e-6
 X_LEAD = 3
 MX_LEAD = 1
+VECTOR_FRAMES = 3
+GPSIMD_HEADS = 6
 
 FLOPS = 2 * TOKENS * K * FEATURES
 
@@ -117,10 +119,10 @@ def tile_causalwanselfattention_pa_kernel(
         nc.vector.tensor_copy(out=b_col[:], in_=b_ps[:, 0, 0, 0:HEADS])
 
         sign = const.tile([P, 2], F32, name="sign")
-        nc.gpsimd.memset(sign[:, 0:1], 1.0)
-        nc.gpsimd.memset(sign[:, 1:2], -1.0)
+        nc.vector.memset(sign[:, 0:1], 1.0)
+        nc.vector.memset(sign[:, 1:2], -1.0)
         g_signed = const.tile([P, FEATURES], F32, name="g_signed")
-        nc.gpsimd.tensor_tensor(
+        nc.vector.tensor_tensor(
             out=g_signed[:].rearrange("p (j i) -> p j i", i=2),
             in0=g_all[:].rearrange("p (j i) -> p j i", i=2),
             in1=sign[:].unsqueeze(1).to_broadcast([P, FEATURES // 2, 2]),
@@ -162,15 +164,18 @@ def tile_causalwanselfattention_pa_kernel(
                     GRID_PAIRS,
                 )
 
-        for f in range(FRAMES):
+        def fill_frame_tables(engine, f):
             for name in ("cos", "sin"):
                 fill_table(
-                    nc.gpsimd,
+                    engine,
                     tab_f[name][:, f, :, :],
                     gain[name][:, :, 0:F_COLS],
                     by_frame[name][:, f * TABLE_PAIRS : f * TABLE_PAIRS + FRAME_PAIRS],
                     FRAME_PAIRS,
                 )
+
+        for f in range(VECTOR_FRAMES, FRAMES):
+            fill_frame_tables(nc.gpsimd, f)
 
         grouped = {}
         codes = {}
@@ -247,6 +252,16 @@ def tile_causalwanselfattention_pa_kernel(
             prod = {}
             for name in ("cos", "sin"):
                 prod[name] = work.tile([P, HEADS, HEAD], F32, name=name + "_prod")
+            rotated = work.tile([P, HEADS, HEAD], F32, name="rotated")
+
+            def add_pairs(engine, heads):
+                engine.tensor_tensor(
+                    out=rotated[:, heads, :].rearrange("p h (j i) -> p (h j) i", i=2),
+                    in0=prod["cos"][:, heads, :].rearrange("p h (j i) -> p (h j) i", i=2),
+                    in1=prod["sin"][:, heads, :].rearrange("p h (j i) -> p (h j) i", i=2)[:, :, ::-1],
+                    op=ALU.add,
+                )
+
             for k in range(BANKS):
                 heads = slice(k * BANK_HEADS, (k + 1) * BANK_HEADS)
                 for name in ("cos", "sin"):
@@ -266,16 +281,15 @@ def tile_causalwanselfattention_pa_kernel(
                         op0=ALU.mult,
                         op1=ALU.mult,
                     )
+                first, last = k * BANK_HEADS, (k + 1) * BANK_HEADS
+                add_pairs(nc.gpsimd, slice(first, min(last, GPSIMD_HEADS)))
+                if last > GPSIMD_HEADS:
+                    add_pairs(nc.vector, slice(max(first, GPSIMD_HEADS), last))
                 if k == 0:
                     between_banks()
-            rotated = work.tile([P, FEATURES], F32, name="rotated")
-            nc.gpsimd.tensor_tensor(
-                out=rotated[:].rearrange("p (j i) -> p j i", i=2),
-                in0=prod["cos"][:].rearrange("p h (j i) -> p (h j) i", i=2),
-                in1=prod["sin"][:].rearrange("p h (j i) -> p (h j) i", i=2)[:, :, ::-1],
-                op=ALU.add,
+            nc.sync.dma_start(
+                out=out_rows[t * P : (t + 1) * P, :], in_=rotated[:].rearrange("p h d -> p (h d)")
             )
-            nc.sync.dma_start(out=out_rows[t * P : (t + 1) * P, :], in_=rotated[:])
 
         for step in range(-X_LEAD, TILES):
             ahead = step + X_LEAD
@@ -292,5 +306,10 @@ def tile_causalwanselfattention_pa_kernel(
                 finish(step, quantise_ahead)
             else:
                 quantise_ahead()
-            if step + 1 in (0, 1):
-                fill_grid_tables(step + 1)
+            if step == -2:
+                fill_grid_tables(0)
+                fill_frame_tables(nc.vector, 0)
+            if step == -1:
+                fill_grid_tables(1)
+                for f in range(1, VECTOR_FRAMES):
+                    fill_frame_tables(nc.vector, f)

@@ -34,8 +34,7 @@ BANKS = FEATURES // BANK
 EPS = 1e-6
 X_LEAD = 3
 MX_LEAD = 1
-VECTOR_FRAMES = 3
-GPSIMD_HEADS = 6
+EARLY_FRAMES = 2
 
 FLOPS = 2 * TOKENS * K * FEATURES
 
@@ -67,7 +66,7 @@ def tile_causalwanselfattention_pa_kernel(
             for name, table in (("cos", freqs_cos), ("sin", freqs_sin)):
                 src = rows(table)
                 pair[name] = const.tile([P, src.shape[-1]], BF16, name="%s_%s" % (name, kind))
-                nc.sync.dma_start(out=pair[name][:], in_=src)
+                nc.gpsimd.dma_start(out=pair[name][:], in_=src)
             return pair
 
         load_x(0)
@@ -85,9 +84,12 @@ def tile_causalwanselfattention_pa_kernel(
             nc.sync.dma_start(
                 out=w_scales[r:P:32, :, :].bitcast(I32), in_=scale_rows[r].bitcast(I32)
             )
+        for t in range(1, TILES):
+            load_x(t)
+        ident = const.tile([P, P], F32, name="ident")
+        make_identity(nc, ident[:])
         g_all = const.tile([P, FEATURES], BF16, name="g_all")
-        nc.sync.dma_start(out=g_all[:], in_=g.partition_broadcast(P))
-        load_x(1)
+        nc.gpsimd.dma_start(out=g_all[:], in_=g.partition_broadcast(P))
         by_col = load_angles(lambda tab: tab.unsqueeze(0).to_broadcast([8, 16, TABLE_PAIRS]), "col")
         by_row = {}
         by_row[0] = load_angles(
@@ -96,16 +98,9 @@ def tile_causalwanselfattention_pa_kernel(
         by_frame = load_angles(
             lambda tab: tab[0:FRAMES, :].rearrange("f j -> (f j)").partition_broadcast(P), "frame"
         )
-        load_x(2)
-        load_x(3)
         by_row[1] = load_angles(
             lambda tab: tab[8:16, :].unsqueeze(1).to_broadcast([8, 16, TABLE_PAIRS]), "row1"
         )
-        for t in range(4, TILES):
-            load_x(t)
-
-        ident = const.tile([P, P], F32, name="ident")
-        make_identity(nc, ident[:])
         eps_col = const.tile([P, 1], F32, name="eps_col")
         nc.vector.memset(eps_col[:], EPS)
         warm = const.tile([P, 1], F32, name="warm")
@@ -139,8 +134,8 @@ def tile_causalwanselfattention_pa_kernel(
             tab_f[name] = const.tile([P, FRAMES, HEADS, F_COLS], F32, name=name + "_tab_f")
         row_end = FRAME_PAIRS + GRID_PAIRS
 
-        def fill_table(engine, dst, gain_cols, angles, pairs):
-            engine.tensor_tensor(
+        def fill_table(dst, gain_cols, angles, pairs):
+            nc.vector.tensor_tensor(
                 out=dst.rearrange("p h (j i) -> p h j i", i=2),
                 in0=gain_cols.rearrange("p h (j i) -> p h j i", i=2),
                 in1=angles.unsqueeze(1).unsqueeze(3).to_broadcast([P, HEADS, pairs, 2]),
@@ -150,32 +145,25 @@ def tile_causalwanselfattention_pa_kernel(
         def fill_grid_tables(half):
             for name in ("cos", "sin"):
                 fill_table(
-                    nc.vector,
                     tab_rc[name][:, half, :, 0 : 2 * GRID_PAIRS],
                     gain[name][:, :, F_COLS : 2 * row_end],
                     by_row[half][name][:, FRAME_PAIRS:row_end],
                     GRID_PAIRS,
                 )
                 fill_table(
-                    nc.vector,
                     tab_rc[name][:, half, :, 2 * GRID_PAIRS : RC_COLS],
                     gain[name][:, :, 2 * row_end : HEAD],
                     by_col[name][:, row_end:TABLE_PAIRS],
                     GRID_PAIRS,
                 )
 
-        def fill_frame_tables(engine, f):
-            for name in ("cos", "sin"):
-                fill_table(
-                    engine,
-                    tab_f[name][:, f, :, :],
-                    gain[name][:, :, 0:F_COLS],
-                    by_frame[name][:, f * TABLE_PAIRS : f * TABLE_PAIRS + FRAME_PAIRS],
-                    FRAME_PAIRS,
-                )
-
-        for f in range(VECTOR_FRAMES, FRAMES):
-            fill_frame_tables(nc.gpsimd, f)
+        def fill_frame_table(name, f):
+            fill_table(
+                tab_f[name][:, f, :, :],
+                gain[name][:, :, 0:F_COLS],
+                by_frame[name][:, f * TABLE_PAIRS : f * TABLE_PAIRS + FRAME_PAIRS],
+                FRAME_PAIRS,
+            )
 
         grouped = {}
         codes = {}
@@ -228,88 +216,85 @@ def tile_causalwanselfattention_pa_kernel(
                         bias=b_col[:, h : h + 1], scale=1.0,
                     )
 
-        def finish(t, between_banks):
-            frame, half = divmod(t, 2)
-            y_ps = [psum_y.tile([P, BANK_HEADS, HEAD], F32, name="y_ps%d" % k) for k in range(BANKS)]
-            for h in range(HEADS):
-                k, hk = divmod(h, BANK_HEADS)
-                nc.tensor.transpose(y_ps[k][:, hk, :], y_feat[t][:, h, :], ident[:])
+        y_ps = {}
+        inv = {}
+
+        def norm(t):
+            for k in range(BANKS):
+                y_ps[t, k] = psum_y.tile([P, BANK_HEADS, HEAD], F32, name="y_ps%d" % k)
+                for hk in range(BANK_HEADS):
+                    nc.tensor.transpose(y_ps[t, k][:, hk, :], y_feat[t][:, k * BANK_HEADS + hk, :], ident[:])
             sums = small.tile([P, BANKS], F32, name="sums")
             for k in range(BANKS):
                 squares = work.tile([P, BANK_HEADS, HEAD], F32, name="squares%d" % k)
                 nc.scalar.activation(
-                    out=squares[:], in_=y_ps[k][:], func=ACT.Square, accum_out=sums[:, k : k + 1]
+                    out=squares[:], in_=y_ps[t, k][:], func=ACT.Square, accum_out=sums[:, k : k + 1]
                 )
             part = small.tile([P, 1], F32, name="part")
             nc.scalar.activation(
                 out=part[:], in_=sums[:, 1:2], func=ACT.Identity, bias=eps_col[:, 0:1], scale=1.0 / FEATURES
             )
-            inv = small.tile([P, 1], F32, name="inv")
+            inv[t] = small.tile([P, 1], F32, name="inv")
             nc.scalar.activation(
-                out=inv[:], in_=sums[:, 0:1], func=ACT.Abs_reciprocal_sqrt, bias=part[:, 0:1],
+                out=inv[t][:], in_=sums[:, 0:1], func=ACT.Abs_reciprocal_sqrt, bias=part[:, 0:1],
                 scale=1.0 / FEATURES,
             )
-            prod = {}
-            for name in ("cos", "sin"):
-                prod[name] = work.tile([P, HEADS, HEAD], F32, name=name + "_prod")
-            rotated = work.tile([P, HEADS, HEAD], F32, name="rotated")
 
-            def add_pairs(engine, heads):
-                engine.tensor_tensor(
-                    out=rotated[:, heads, :].rearrange("p h (j i) -> p (h j) i", i=2),
-                    in0=prod["cos"][:, heads, :].rearrange("p h (j i) -> p (h j) i", i=2),
-                    in1=prod["sin"][:, heads, :].rearrange("p h (j i) -> p (h j) i", i=2)[:, :, ::-1],
-                    op=ALU.add,
-                )
-
+        def rotate(t):
+            frame, half = divmod(t, 2)
             for k in range(BANKS):
                 heads = slice(k * BANK_HEADS, (k + 1) * BANK_HEADS)
+                prod = {}
                 for name in ("cos", "sin"):
+                    prod[name] = work.tile([P, BANK_HEADS, HEAD], F32, name="%s_prod%d" % (name, k))
                     nc.vector.scalar_tensor_tensor(
-                        out=prod[name][:, heads, 0:F_COLS],
-                        in0=y_ps[k][:, :, 0:F_COLS],
-                        scalar=inv[:, 0:1],
+                        out=prod[name][:, :, 0:F_COLS],
+                        in0=y_ps[t, k][:, :, 0:F_COLS],
+                        scalar=inv[t][:, 0:1],
                         in1=tab_f[name][:, frame, heads, :],
                         op0=ALU.mult,
                         op1=ALU.mult,
                     )
                     nc.vector.scalar_tensor_tensor(
-                        out=prod[name][:, heads, F_COLS:HEAD],
-                        in0=y_ps[k][:, :, F_COLS:HEAD],
-                        scalar=inv[:, 0:1],
+                        out=prod[name][:, :, F_COLS:HEAD],
+                        in0=y_ps[t, k][:, :, F_COLS:HEAD],
+                        scalar=inv[t][:, 0:1],
                         in1=tab_rc[name][:, half, heads, :],
                         op0=ALU.mult,
                         op1=ALU.mult,
                     )
-                first, last = k * BANK_HEADS, (k + 1) * BANK_HEADS
-                add_pairs(nc.gpsimd, slice(first, min(last, GPSIMD_HEADS)))
-                if last > GPSIMD_HEADS:
-                    add_pairs(nc.vector, slice(max(first, GPSIMD_HEADS), last))
-                if k == 0:
-                    between_banks()
-            nc.sync.dma_start(
-                out=out_rows[t * P : (t + 1) * P, :], in_=rotated[:].rearrange("p h d -> p (h d)")
-            )
+                rotated = work.tile([P, BANK], F32, name="rotated%d" % k)
+                nc.gpsimd.tensor_tensor(
+                    out=rotated[:].rearrange("p (j i) -> p j i", i=2),
+                    in0=prod["cos"][:].rearrange("p h (j i) -> p (h j) i", i=2),
+                    in1=prod["sin"][:].rearrange("p h (j i) -> p (h j) i", i=2)[:, :, ::-1],
+                    op=ALU.add,
+                )
+                nc.sync.dma_start(
+                    out=out_rows[t * P : (t + 1) * P, k * BANK : (k + 1) * BANK], in_=rotated[:]
+                )
 
         for step in range(-X_LEAD, TILES):
-            ahead = step + X_LEAD
-
-            def quantise_ahead():
-                if ahead < TILES:
-                    quantise_x(ahead)
-
-            if ahead < TILES:
-                transpose_x(ahead)
+            if step + X_LEAD < TILES:
+                transpose_x(step + X_LEAD)
+            if step >= 0:
+                norm(step)
             if 0 <= step + MX_LEAD < TILES:
                 project(step + MX_LEAD)
             if step >= 0:
-                finish(step, quantise_ahead)
-            else:
-                quantise_ahead()
-            if step == -2:
+                rotate(step)
+            if step + X_LEAD < TILES:
+                quantise_x(step + X_LEAD)
+            if step == -X_LEAD:
                 fill_grid_tables(0)
-                fill_frame_tables(nc.vector, 0)
-            if step == -1:
+            if step == -X_LEAD + 1:
+                fill_frame_table("cos", 0)
+                fill_frame_table("sin", 0)
+            if step == -X_LEAD + 2:
                 fill_grid_tables(1)
-                for f in range(1, VECTOR_FRAMES):
-                    fill_frame_tables(nc.vector, f)
+                for f in range(1, EARLY_FRAMES):
+                    fill_frame_table("cos", f)
+                    fill_frame_table("sin", f)
+            late_frame = EARLY_FRAMES + step // 2
+            if step >= 0 and late_frame < FRAMES:
+                fill_frame_table(("cos", "sin")[step % 2], late_frame)

@@ -32,9 +32,13 @@ BANK = 512
 BANK_HEADS = BANK // HEAD
 BANKS = FEATURES // BANK
 EPS = 1e-6
-X_LEAD = 3
-MX_LEAD = 1
-EARLY_FRAMES = 2
+BLOCK_TILES = 4
+BLOCK = BLOCK_TILES * P
+BLOCKS = TILES // BLOCK_TILES
+STEP_HEADS = HEADS // BLOCK_TILES
+X_LEAD = 2 * BLOCK_TILES
+MX_LEAD = BLOCK_TILES
+EARLY_FRAMES = 4
 
 FLOPS = 2 * TOKENS * K * FEATURES
 
@@ -48,12 +52,12 @@ def tile_causalwanselfattention_pa_kernel(
 
     with ExitStack() as ctx:
         const = ctx.enter_context(tc.tile_pool(name="const", bufs=1))
-        quant = ctx.enter_context(tc.tile_pool(name="quant", bufs=3))
+        quant = ctx.enter_context(tc.tile_pool(name="quant", bufs=4))
         feat = ctx.enter_context(tc.tile_pool(name="feat", bufs=2))
         work = ctx.enter_context(tc.tile_pool(name="work", bufs=3))
         small = ctx.enter_context(tc.tile_pool(name="small", bufs=4))
         psum_x = ctx.enter_context(tc.psum_pool(name="psum_x", bufs=2))
-        psum_a = ctx.enter_context(tc.psum_pool(name="psum_a", bufs=1))
+        psum_a = ctx.enter_context(tc.psum_pool(name="psum_a", bufs=2))
         psum_y = ctx.enter_context(tc.psum_pool(name="psum_y", bufs=2))
         ctx.enter_context(tc.manual_schedule())
         x_tiles = [const.tile([P, K], BF16, name="x%d" % t) for t in range(TILES)]
@@ -69,14 +73,12 @@ def tile_causalwanselfattention_pa_kernel(
                 nc.gpsimd.dma_start(out=pair[name][:], in_=src)
             return pair
 
-        load_x(0)
         b_rows = const.tile([P, P], BF16, name="b_rows")
         nc.vector.memset(b_rows[:], 0.0)
         nc.sync.dma_start(out=b_rows[0:HEADS, :], in_=b.rearrange("(h d) -> h d", d=HEAD))
+        for t in range(BLOCK_TILES + 1):
+            load_x(t)
         w_words = const.tile([P, PASSES, 2 * FEATURES], U8, name="w_words", align_bytes=64)
-        nc.sync.dma_start(
-            out=w_words[:].bitcast(I32), in_=W_words.rearrange("c p n -> p c n").bitcast(I32)
-        )
         w_scales = const.tile([P, PASSES, FEATURES], U8, name="w_scales", align_bytes=64)
         nc.vector.memset(w_scales[:].bitcast(I32), 0)
         scale_rows = W_scales.rearrange("c (q r) n -> r q c n", r=4)
@@ -84,7 +86,16 @@ def tile_causalwanselfattention_pa_kernel(
             nc.sync.dma_start(
                 out=w_scales[r:P:32, :, :].bitcast(I32), in_=scale_rows[r].bitcast(I32)
             )
-        for t in range(1, TILES):
+        words_src = W_words.rearrange("c p n -> p c n")
+        piece = 2 * HEAD * STEP_HEADS
+        for i in range(BLOCK_TILES):
+            nc.sync.dma_start(
+                out=w_words[:, :, i * piece : (i + 1) * piece].bitcast(I32),
+                in_=words_src[:, :, i * piece : (i + 1) * piece].bitcast(I32),
+            )
+            if i > 0:
+                load_x(BLOCK_TILES + i)
+        for t in range(2 * BLOCK_TILES, TILES):
             load_x(t)
         ident = const.tile([P, P], F32, name="ident")
         make_identity(nc, ident[:])
@@ -117,12 +128,15 @@ def tile_causalwanselfattention_pa_kernel(
         nc.vector.memset(sign[:, 0:1], 1.0)
         nc.vector.memset(sign[:, 1:2], -1.0)
         g_signed = const.tile([P, FEATURES], F32, name="g_signed")
-        nc.vector.tensor_tensor(
-            out=g_signed[:].rearrange("p (j i) -> p j i", i=2),
-            in0=g_all[:].rearrange("p (j i) -> p j i", i=2),
-            in1=sign[:].unsqueeze(1).to_broadcast([P, FEATURES // 2, 2]),
-            op=ALU.mult,
-        )
+
+        def fill_signed_gain():
+            nc.vector.tensor_tensor(
+                out=g_signed[:].rearrange("p (j i) -> p j i", i=2),
+                in0=g_all[:].rearrange("p (j i) -> p j i", i=2),
+                in1=sign[:].unsqueeze(1).to_broadcast([P, FEATURES // 2, 2]),
+                op=ALU.mult,
+            )
+
         gain = {
             "cos": g_all[:].rearrange("p (h d) -> p h d", d=HEAD),
             "sin": g_signed[:].rearrange("p (h d) -> p h d", d=HEAD),
@@ -134,8 +148,8 @@ def tile_causalwanselfattention_pa_kernel(
             tab_f[name] = const.tile([P, FRAMES, HEADS, F_COLS], F32, name=name + "_tab_f")
         row_end = FRAME_PAIRS + GRID_PAIRS
 
-        def fill_table(dst, gain_cols, angles, pairs):
-            nc.vector.tensor_tensor(
+        def fill_table(dst, gain_cols, angles, pairs, engine=nc.vector):
+            engine.tensor_tensor(
                 out=dst.rearrange("p h (j i) -> p h j i", i=2),
                 in0=gain_cols.rearrange("p h (j i) -> p h j i", i=2),
                 in1=angles.unsqueeze(1).unsqueeze(3).to_broadcast([P, HEADS, pairs, 2]),
@@ -157,17 +171,18 @@ def tile_causalwanselfattention_pa_kernel(
                     GRID_PAIRS,
                 )
 
-        def fill_frame_table(name, f):
+        def fill_frame_table(name, f, engine=nc.vector):
             fill_table(
                 tab_f[name][:, f, :, :],
                 gain[name][:, :, 0:F_COLS],
                 by_frame[name][:, f * TABLE_PAIRS : f * TABLE_PAIRS + FRAME_PAIRS],
                 FRAME_PAIRS,
+                engine,
             )
 
         grouped = {}
-        codes = {}
-        planes = {}
+        codes = [const.tile([P, PASSES, BLOCK], U32, name="codes%d" % blk, align_bytes=64) for blk in range(BLOCKS)]
+        planes = [const.tile([P, PASSES, BLOCK], U8, name="planes%d" % blk, align_bytes=64) for blk in range(BLOCKS)]
         y_feat = {}
 
         def transpose_x(t):
@@ -185,58 +200,62 @@ def tile_causalwanselfattention_pa_kernel(
             )
 
         def quantise_x(t):
-            codes[t] = quant.tile([P, PASSES, P], U32, name="codes", align_bytes=64)
-            planes[t] = quant.tile([P, PASSES, P], U8, name="planes", align_bytes=64)
-            nc.vector.quantize_mx(
-                out=codes[t][:].rearrange("p c r -> p (c r)").bitcast(FP8X4),
-                scales=planes[t][:].rearrange("p c r -> p (c r)"),
-                in_=grouped[t][:],
-            )
+            blk, i = divmod(t, BLOCK_TILES)
+            for c in range(PASSES):
+                nc.vector.quantize_mx(
+                    out=codes[blk][:, c, i * P : (i + 1) * P].bitcast(FP8X4),
+                    scales=planes[blk][:, c, i * P : (i + 1) * P],
+                    in_=grouped[t][:, c * 4 * P : (c + 1) * 4 * P],
+                )
 
-        def project(t):
-            acc = [psum_a.tile([P, BANK_HEADS, P], F32, name="acc%d" % k) for k in range(BANKS)]
-            y_feat[t] = feat.tile([P, HEADS, P], F32, name="y_feat")
-            for k in range(BANKS):
-                for hk in range(BANK_HEADS):
-                    h = k * BANK_HEADS + hk
-                    for c in range(PASSES):
-                        nc.tensor.matmul_mx(
-                            out=acc[k][:, hk, :],
-                            lhsT=w_words[:, c, 2 * HEAD * h : 2 * HEAD * (h + 1)].bitcast(FP4X4),
-                            lhsT_scale=w_scales[:, c, HEAD * h : HEAD * (h + 1)],
-                            rhs=codes[t][:, c, :].bitcast(FP8X4),
-                            rhs_scale=planes[t][:, c, :],
-                            start=(c == 0),
-                            stop=(c == PASSES - 1),
-                        )
-                for hk in range(BANK_HEADS):
-                    h = k * BANK_HEADS + hk
-                    nc.scalar.activation(
-                        out=y_feat[t][:, h, :], in_=acc[k][:, hk, :], func=ACT.Identity,
-                        bias=b_col[:, h : h + 1], scale=1.0,
-                    )
+        def project(blk, h):
+            if h == 0:
+                y_feat[blk] = feat.tile([P, HEADS, BLOCK], F32, name="y_feat")
+            acc = psum_a.tile([P, BLOCK], F32, name="acc")
+            for c in range(PASSES):
+                nc.tensor.matmul_mx(
+                    out=acc[:],
+                    lhsT=w_words[:, c, 2 * HEAD * h : 2 * HEAD * (h + 1)].bitcast(FP4X4),
+                    lhsT_scale=w_scales[:, c, HEAD * h : HEAD * (h + 1)],
+                    rhs=codes[blk][:, c, :].bitcast(FP8X4),
+                    rhs_scale=planes[blk][:, c, :],
+                    start=(c == 0),
+                    stop=(c == PASSES - 1),
+                )
+            nc.scalar.activation(
+                out=y_feat[blk][:, h, :], in_=acc[:], func=ACT.Identity, bias=b_col[:, h : h + 1], scale=1.0
+            )
 
         y_ps = {}
+        sums = {}
         inv = {}
 
-        def norm(t):
-            for k in range(BANKS):
-                y_ps[t, k] = psum_y.tile([P, BANK_HEADS, HEAD], F32, name="y_ps%d" % k)
-                for hk in range(BANK_HEADS):
-                    nc.tensor.transpose(y_ps[t, k][:, hk, :], y_feat[t][:, k * BANK_HEADS + hk, :], ident[:])
-            sums = small.tile([P, BANKS], F32, name="sums")
-            for k in range(BANKS):
-                squares = work.tile([P, BANK_HEADS, HEAD], F32, name="squares%d" % k)
-                nc.scalar.activation(
-                    out=squares[:], in_=y_ps[t, k][:], func=ACT.Square, accum_out=sums[:, k : k + 1]
+        def back(t, k):
+            blk, i = divmod(t, BLOCK_TILES)
+            y_ps[t, k] = psum_y.tile([P, BANK_HEADS, HEAD], F32, name="y_ps%d" % k)
+            for hk in range(BANK_HEADS):
+                nc.tensor.transpose(
+                    y_ps[t, k][:, hk, :], y_feat[blk][:, k * BANK_HEADS + hk, i * P : (i + 1) * P], ident[:]
                 )
-            part = small.tile([P, 1], F32, name="part")
+            if k == 0:
+                sums[t] = small.tile([P, BANKS], F32, name="sums")
+            squares = work.tile([P, BANK_HEADS, HEAD], F32, name="squares%d" % k)
             nc.scalar.activation(
-                out=part[:], in_=sums[:, 1:2], func=ACT.Identity, bias=eps_col[:, 0:1], scale=1.0 / FEATURES
+                out=squares[:], in_=y_ps[t, k][:], func=ACT.Square, accum_out=sums[t][:, k : k + 1]
             )
+
+        part = {}
+
+        def norm_first(t):
+            part[t] = small.tile([P, 1], F32, name="part")
+            nc.scalar.activation(
+                out=part[t][:], in_=sums[t][:, 0:1], func=ACT.Identity, bias=eps_col[:, 0:1], scale=1.0 / FEATURES
+            )
+
+        def norm(t):
             inv[t] = small.tile([P, 1], F32, name="inv")
             nc.scalar.activation(
-                out=inv[t][:], in_=sums[:, 0:1], func=ACT.Abs_reciprocal_sqrt, bias=part[:, 0:1],
+                out=inv[t][:], in_=sums[t][:, 1:2], func=ACT.Abs_reciprocal_sqrt, bias=part[t][:, 0:1],
                 scale=1.0 / FEATURES,
             )
 
@@ -275,26 +294,37 @@ def tile_causalwanselfattention_pa_kernel(
                 )
 
         for step in range(-X_LEAD, TILES):
-            if step + X_LEAD < TILES:
-                transpose_x(step + X_LEAD)
+            ahead = step + X_LEAD
+            blk, i = divmod(step + MX_LEAD, BLOCK_TILES)
+            projecting = 0 <= blk < BLOCKS
             if step >= 0:
+                back(step, 0)
+                back(step, 1)
+                norm_first(step)
+            if ahead < TILES:
+                transpose_x(ahead)
+            if step >= 0 and (ahead < TILES or not projecting):
                 norm(step)
-            if 0 <= step + MX_LEAD < TILES:
-                project(step + MX_LEAD)
+            if projecting:
+                project(blk, STEP_HEADS * i)
+                if step >= 0 and ahead >= TILES:
+                    norm(step)
+                project(blk, STEP_HEADS * i + 1)
+            if ahead < TILES:
+                quantise_x(ahead)
             if step >= 0:
                 rotate(step)
-            if step + X_LEAD < TILES:
-                quantise_x(step + X_LEAD)
-            if step == -X_LEAD:
-                fill_grid_tables(0)
-            if step == -X_LEAD + 1:
-                fill_frame_table("cos", 0)
-                fill_frame_table("sin", 0)
-            if step == -X_LEAD + 2:
-                fill_grid_tables(1)
-                for f in range(1, EARLY_FRAMES):
-                    fill_frame_table("cos", f)
-                    fill_frame_table("sin", f)
+            if step == -MX_LEAD - 1:
+                fill_signed_gain()
+            plan = {-4: ("g0",), -3: (0, 1), -2: ("g1",), -1: (2, 3)}.get(step, ())
+            for item in plan:
+                if item == "g0":
+                    fill_grid_tables(0)
+                elif item == "g1":
+                    fill_grid_tables(1)
+                else:
+                    fill_frame_table("cos", item)
+                    fill_frame_table("sin", item)
             late_frame = EARLY_FRAMES + step // 2
             if step >= 0 and late_frame < FRAMES:
                 fill_frame_table(("cos", "sin")[step % 2], late_frame)

@@ -38,6 +38,7 @@ BLOCKS = TILES // BLOCK_TILES
 STEP_HEADS = HEADS // BLOCK_TILES
 X_LEAD = 2 * BLOCK_TILES
 MX_LEAD = BLOCK_TILES
+ADDS_LAST = 2
 EARLY_FRAMES = 4
 
 FLOPS = 2 * TOKENS * K * FEATURES
@@ -261,13 +262,12 @@ def tile_causalwanselfattention_pa_kernel(
 
         def rotate(t):
             frame, half = divmod(t, 2)
+            prod = {name: work.tile([P, HEADS, HEAD], F32, name=name + "_prod") for name in ("cos", "sin")}
             for k in range(BANKS):
                 heads = slice(k * BANK_HEADS, (k + 1) * BANK_HEADS)
-                prod = {}
                 for name in ("cos", "sin"):
-                    prod[name] = work.tile([P, BANK_HEADS, HEAD], F32, name="%s_prod%d" % (name, k))
                     nc.vector.scalar_tensor_tensor(
-                        out=prod[name][:, :, 0:F_COLS],
+                        out=prod[name][:, heads, 0:F_COLS],
                         in0=y_ps[t, k][:, :, 0:F_COLS],
                         scalar=inv[t][:, 0:1],
                         in1=tab_f[name][:, frame, heads, :],
@@ -275,23 +275,25 @@ def tile_causalwanselfattention_pa_kernel(
                         op1=ALU.mult,
                     )
                     nc.vector.scalar_tensor_tensor(
-                        out=prod[name][:, :, F_COLS:HEAD],
+                        out=prod[name][:, heads, F_COLS:HEAD],
                         in0=y_ps[t, k][:, :, F_COLS:HEAD],
                         scalar=inv[t][:, 0:1],
                         in1=tab_rc[name][:, half, heads, :],
                         op0=ALU.mult,
                         op1=ALU.mult,
                     )
-                rotated = work.tile([P, BANK], F32, name="rotated%d" % k)
+            rotated = work.tile([P, FEATURES], F32, name="rotated")
+            pieces = ADDS_LAST if t == TILES - 1 else 1
+            width = FEATURES // pieces
+            for n in range(pieces):
+                cols = slice(n * width, (n + 1) * width)
                 nc.gpsimd.tensor_tensor(
-                    out=rotated[:].rearrange("p (j i) -> p j i", i=2),
-                    in0=prod["cos"][:].rearrange("p h (j i) -> p (h j) i", i=2),
-                    in1=prod["sin"][:].rearrange("p h (j i) -> p (h j) i", i=2)[:, :, ::-1],
+                    out=rotated[:, cols].rearrange("p (j i) -> p j i", i=2),
+                    in0=prod["cos"][:].rearrange("p h d -> p (h d)")[:, cols].rearrange("p (j i) -> p j i", i=2),
+                    in1=prod["sin"][:].rearrange("p h d -> p (h d)")[:, cols].rearrange("p (j i) -> p j i", i=2)[:, :, ::-1],
                     op=ALU.add,
                 )
-                nc.sync.dma_start(
-                    out=out_rows[t * P : (t + 1) * P, k * BANK : (k + 1) * BANK], in_=rotated[:]
-                )
+                nc.sync.dma_start(out=out_rows[t * P : (t + 1) * P, cols], in_=rotated[:, cols])
 
         for step in range(-X_LEAD, TILES):
             ahead = step + X_LEAD

@@ -29,6 +29,7 @@ TABLE_PAIRS = 64
 F_COLS = 2 * FRAME_PAIRS
 RC_COLS = HEAD - F_COLS
 BANK = 512
+BANK_BYTES = 4 * BANK
 BANK_HEADS = BANK // HEAD
 BANKS = FEATURES // BANK
 EPS = 1e-6
@@ -36,10 +37,16 @@ BLOCK_TILES = 4
 BLOCK = BLOCK_TILES * P
 BLOCKS = TILES // BLOCK_TILES
 STEP_HEADS = HEADS // BLOCK_TILES
-X_LEAD = 2 * BLOCK_TILES
+X_LEAD = 2 * BLOCK_TILES + 1
 MX_LEAD = BLOCK_TILES
 ADDS_LAST = 2
 EARLY_FRAMES = 4
+
+X_BANKS = (0, 1)
+ACC_BANKS = (2, 3)
+Y_BANKS = (4, 5, 6, 7)
+FIRST_X_BANKS = (0, 1, 4, 5)
+FIRST_ACC_BANKS = (2, 3, 6, 7, 4, 5)
 
 FLOPS = 2 * TOKENS * K * FEATURES
 
@@ -53,13 +60,17 @@ def tile_causalwanselfattention_pa_kernel(
 
     with ExitStack() as ctx:
         const = ctx.enter_context(tc.tile_pool(name="const", bufs=1))
-        quant = ctx.enter_context(tc.tile_pool(name="quant", bufs=4))
+        quant = ctx.enter_context(tc.tile_pool(name="quant", bufs=6))
         feat = ctx.enter_context(tc.tile_pool(name="feat", bufs=2))
         work = ctx.enter_context(tc.tile_pool(name="work", bufs=3))
         small = ctx.enter_context(tc.tile_pool(name="small", bufs=4))
-        psum_x = ctx.enter_context(tc.psum_pool(name="psum_x", bufs=2))
-        psum_a = ctx.enter_context(tc.psum_pool(name="psum_a", bufs=2))
-        psum_y = ctx.enter_context(tc.psum_pool(name="psum_y", bufs=2))
+        psum = ctx.enter_context(tc.psum_pool(name="psum", bufs=1))
+        made = []
+
+        def bank_tile(bank, shape, label):
+            made.append(label)
+            return psum.tile(shape, F32, name="%s_%d" % (label, len(made)), offset=bank * BANK_BYTES)
+
         ctx.enter_context(tc.manual_schedule())
         x_tiles = [const.tile([P, K], BF16, name="x%d" % t) for t in range(TILES)]
 
@@ -76,8 +87,9 @@ def tile_causalwanselfattention_pa_kernel(
 
         b_rows = const.tile([P, P], BF16, name="b_rows")
         nc.vector.memset(b_rows[:], 0.0)
+        load_x(0)
         nc.sync.dma_start(out=b_rows[0:HEADS, :], in_=b.rearrange("(h d) -> h d", d=HEAD))
-        for t in range(BLOCK_TILES + 1):
+        for t in range(1, BLOCK_TILES + 1):
             load_x(t)
         w_words = const.tile([P, PASSES, 2 * FEATURES], U8, name="w_words", align_bytes=64)
         w_scales = const.tile([P, PASSES, FEATURES], U8, name="w_scales", align_bytes=64)
@@ -120,10 +132,13 @@ def tile_causalwanselfattention_pa_kernel(
 
         b_rows32 = const.tile([P, P], F32, name="b_rows32")
         nc.vector.tensor_copy(out=b_rows32[:], in_=b_rows[:])
-        b_ps = psum_x.tile([P, PASSES, 2, P], F32, name="b_ps", tag="xt")
-        nc.tensor.transpose(b_ps[:, 0, 0, :], b_rows32[:], ident[:])
         b_col = const.tile([P, HEADS], F32, name="b_col")
-        nc.vector.tensor_copy(out=b_col[:], in_=b_ps[:, 0, 0, 0:HEADS])
+
+        def turn_bias():
+            b_ps = bank_tile(7, [P, P], "b_ps")
+            nc.tensor.transpose(b_ps[:], b_rows32[:], ident[:])
+            nc.vector.tensor_copy(out=b_col[:], in_=b_ps[:, 0:HEADS])
+
 
         sign = const.tile([P, 2], F32, name="sign")
         nc.vector.memset(sign[:, 0:1], 1.0)
@@ -188,7 +203,7 @@ def tile_causalwanselfattention_pa_kernel(
 
         def transpose_x(t):
             x_words = x_tiles[t][:].bitcast(F32)
-            xt = psum_x.tile([P, PASSES, 2, P], F32, name="xt")
+            xt = bank_tile(FIRST_X_BANKS[t] if t < len(FIRST_X_BANKS) else X_BANKS[t % len(X_BANKS)], [P, PASSES, 2, P], "xt")
             for c in range(PASSES):
                 for u in range(2):
                     nc.tensor.transpose(
@@ -212,7 +227,8 @@ def tile_causalwanselfattention_pa_kernel(
         def project(blk, h):
             if h == 0:
                 y_feat[blk] = feat.tile([P, HEADS, BLOCK], F32, name="y_feat")
-            acc = psum_a.tile([P, BLOCK], F32, name="acc")
+            banks = FIRST_ACC_BANKS if blk == 0 else ACC_BANKS
+            acc = bank_tile(banks[h % len(banks)], [P, BLOCK], "acc")
             for c in range(PASSES):
                 nc.tensor.matmul_mx(
                     out=acc[:],
@@ -233,7 +249,7 @@ def tile_causalwanselfattention_pa_kernel(
 
         def back(t, k):
             blk, i = divmod(t, BLOCK_TILES)
-            y_ps[t, k] = psum_y.tile([P, BANK_HEADS, HEAD], F32, name="y_ps%d" % k)
+            y_ps[t, k] = bank_tile(Y_BANKS[BANKS * (t % 2) + k], [P, BANK_HEADS, HEAD], "y_ps")
             for hk in range(BANK_HEADS):
                 nc.tensor.transpose(
                     y_ps[t, k][:, hk, :], y_feat[blk][:, k * BANK_HEADS + hk, i * P : (i + 1) * P], ident[:]
@@ -287,7 +303,7 @@ def tile_causalwanselfattention_pa_kernel(
             width = FEATURES // pieces
             for n in range(pieces):
                 cols = slice(n * width, (n + 1) * width)
-                nc.gpsimd.tensor_tensor(
+                (nc.vector if t == TILES - 1 else nc.gpsimd).tensor_tensor(
                     out=rotated[:, cols].rearrange("p (j i) -> p j i", i=2),
                     in0=prod["cos"][:].rearrange("p h d -> p (h d)")[:, cols].rearrange("p (j i) -> p j i", i=2),
                     in1=prod["sin"][:].rearrange("p h d -> p (h d)")[:, cols].rearrange("p (j i) -> p j i", i=2)[:, :, ::-1],
@@ -295,38 +311,46 @@ def tile_causalwanselfattention_pa_kernel(
                 )
                 nc.sync.dma_start(out=out_rows[t * P : (t + 1) * P, cols], in_=rotated[:, cols])
 
-        for step in range(-X_LEAD, TILES):
+        for t in range(BLOCK_TILES):
+            transpose_x(t)
+            if t == 1:
+                turn_bias()
+            quantise_x(t)
+        fill_signed_gain()
+        fill_grid_tables(0)
+        early_x = ((4, 5), (6, 7, 8))
+        early_frames = ((1, 2), (3,))
+        for stage in range(2):
+            for h in range(BANK_HEADS * stage, BANK_HEADS * (stage + 1)):
+                project(0, h)
+            for t in early_x[stage]:
+                transpose_x(t)
+            if stage == 0:
+                fill_frame_table("cos", 0)
+                fill_frame_table("sin", 0)
+                fill_grid_tables(1)
+            for t in early_x[stage]:
+                quantise_x(t)
+            for f in early_frames[stage]:
+                fill_frame_table("cos", f)
+                fill_frame_table("sin", f)
+        for step in range(TILES):
             ahead = step + X_LEAD
             blk, i = divmod(step + MX_LEAD, BLOCK_TILES)
-            projecting = 0 <= blk < BLOCKS
-            if step >= 0:
-                back(step, 0)
-                back(step, 1)
-                norm_first(step)
-            if ahead < TILES:
+            back(step, 0)
+            back(step, 1)
+            norm_first(step)
+            if ahead < TILES and step > 0:
                 transpose_x(ahead)
-            if step >= 0 and (ahead < TILES or not projecting):
-                norm(step)
-            if projecting:
-                project(blk, STEP_HEADS * i)
-                if step >= 0 and ahead >= TILES:
-                    norm(step)
-                project(blk, STEP_HEADS * i + 1)
+            norm(step)
+            if ahead < TILES and step == 0:
+                transpose_x(ahead)
+            if blk < BLOCKS:
+                for n in range(STEP_HEADS):
+                    project(blk, STEP_HEADS * i + n)
+            rotate(step)
             if ahead < TILES:
                 quantise_x(ahead)
-            if step >= 0:
-                rotate(step)
-            if step == -MX_LEAD - 1:
-                fill_signed_gain()
-            plan = {-4: ("g0",), -3: (0, 1), -2: ("g1",), -1: (2, 3)}.get(step, ())
-            for item in plan:
-                if item == "g0":
-                    fill_grid_tables(0)
-                elif item == "g1":
-                    fill_grid_tables(1)
-                else:
-                    fill_frame_table("cos", item)
-                    fill_frame_table("sin", item)
             late_frame = EARLY_FRAMES + step // 2
-            if step >= 0 and late_frame < FRAMES:
+            if late_frame < FRAMES:
                 fill_frame_table(("cos", "sin")[step % 2], late_frame)

@@ -85,6 +85,8 @@ def tile_causalwanselfattention_pa_kernel(
                 nc.gpsimd.dma_start(out=pair[name][:], in_=src)
             return pair
 
+        g_few = const.tile([FRAMES, FEATURES], BF16, name="g_few")
+        frame_rows = {name: const.tile([FRAMES, TABLE_PAIRS], BF16, name=name + "_frame_rows") for name in ("cos", "sin")}
         b_rows = const.tile([P, P], BF16, name="b_rows")
         nc.vector.memset(b_rows[:], 0.0)
         load_x(0)
@@ -110,6 +112,9 @@ def tile_causalwanselfattention_pa_kernel(
                 load_x(BLOCK_TILES + i)
         for t in range(2 * BLOCK_TILES, TILES):
             load_x(t)
+        nc.sync.dma_start(out=g_few[:], in_=g.partition_broadcast(FRAMES))
+        nc.sync.dma_start(out=frame_rows["cos"][:], in_=freqs_cos[0:FRAMES, :])
+        nc.sync.dma_start(out=frame_rows["sin"][:], in_=freqs_sin[0:FRAMES, :])
         ident = const.tile([P, P], F32, name="ident")
         make_identity(nc, ident[:])
         g_all = const.tile([P, FEATURES], BF16, name="g_all")
@@ -120,7 +125,7 @@ def tile_causalwanselfattention_pa_kernel(
             lambda tab: tab[0:8, :].unsqueeze(1).to_broadcast([8, 16, TABLE_PAIRS]), "row0"
         )
         by_frame = load_angles(
-            lambda tab: tab[0:FRAMES, :].rearrange("f j -> (f j)").partition_broadcast(P), "frame"
+            lambda tab: tab[0:EARLY_FRAMES, :].rearrange("f j -> (f j)").partition_broadcast(P), "frame"
         )
         by_row[1] = load_angles(
             lambda tab: tab[8:16, :].unsqueeze(1).to_broadcast([8, 16, TABLE_PAIRS]), "row1"
@@ -161,8 +166,36 @@ def tile_causalwanselfattention_pa_kernel(
         tab_f = {}
         for name in ("cos", "sin"):
             tab_rc[name] = const.tile([P, 2, HEADS, RC_COLS], F32, name=name + "_tab_rc")
-            tab_f[name] = const.tile([P, FRAMES, HEADS, F_COLS], F32, name=name + "_tab_f")
         row_end = FRAME_PAIRS + GRID_PAIRS
+        FRAME_TABLE = 2 * HEADS * F_COLS
+        few = const.tile([FRAMES, 2, HEADS, F_COLS], F32, name="few")
+        tab_frames = const.tile([P, FRAMES, 2, HEADS, F_COLS], F32, name="tab_frames")
+        for n, name in enumerate(("cos", "sin")):
+            tab_f[name] = tab_frames[:, :, n, :, :]
+        parked = out_rows[TOKENS - FRAMES : TOKENS, 0:FRAME_TABLE]
+
+        def park_frame_tables():
+            for n, name in enumerate(("cos", "sin")):
+                angles = frame_rows[name][:, 0:FRAME_PAIRS].unsqueeze(2).to_broadcast([FRAMES, FRAME_PAIRS, 2])
+                if name == "sin":
+                    signed = const.tile([FRAMES, FRAME_PAIRS, 2], F32, name="signed_few")
+                    nc.vector.tensor_tensor(
+                        out=signed[:], in0=angles,
+                        in1=sign[0:FRAMES, :].unsqueeze(1).to_broadcast([FRAMES, FRAME_PAIRS, 2]), op=ALU.mult,
+                    )
+                    angles = signed[:]
+                nc.vector.tensor_tensor(
+                    out=few[:, n, :, :].rearrange("p h (j i) -> p h j i", i=2),
+                    in0=g_few[:].rearrange("p (h d) -> p h d", d=HEAD)[:, :, 0:F_COLS].rearrange("p h (j i) -> p h j i", i=2),
+                    in1=angles.unsqueeze(1).to_broadcast([FRAMES, HEADS, FRAME_PAIRS, 2]),
+                    op=ALU.mult,
+                )
+            nc.sync.dma_start(out=parked, in_=few[:].rearrange("p n h d -> p (n h d)"))
+            nc.sync.dma_start(
+                out=tab_frames[:, EARLY_FRAMES:FRAMES, :, :, :].rearrange("p f n h d -> p f (n h d)"),
+                in_=parked[EARLY_FRAMES:FRAMES, :].unsqueeze(0).to_broadcast([P, FRAMES - EARLY_FRAMES, FRAME_TABLE]),
+            )
+
 
         def fill_table(dst, gain_cols, angles, pairs, engine=nc.vector):
             engine.tensor_tensor(
@@ -318,7 +351,8 @@ def tile_causalwanselfattention_pa_kernel(
             quantise_x(t)
         fill_signed_gain()
         fill_grid_tables(0)
-        early_x = ((4, 5), (6, 7, 8))
+        early_x = ((4, 5), (6, 7))
+        late_x = (8,)
         early_frames = ((1, 2), (3,))
         for stage in range(2):
             for h in range(BANK_HEADS * stage, BANK_HEADS * (stage + 1)):
@@ -334,6 +368,8 @@ def tile_causalwanselfattention_pa_kernel(
             for f in early_frames[stage]:
                 fill_frame_table("cos", f)
                 fill_frame_table("sin", f)
+            if stage == 1:
+                park_frame_tables()
         for step in range(TILES):
             ahead = step + X_LEAD
             blk, i = divmod(step + MX_LEAD, BLOCK_TILES)
@@ -343,14 +379,16 @@ def tile_causalwanselfattention_pa_kernel(
             if ahead < TILES and step > 0:
                 transpose_x(ahead)
             norm(step)
-            if ahead < TILES and step == 0:
+            if step == 0:
+                for t in late_x:
+                    transpose_x(t)
                 transpose_x(ahead)
             if blk < BLOCKS:
                 for n in range(STEP_HEADS):
                     project(blk, STEP_HEADS * i + n)
             rotate(step)
+            if step == 0:
+                for t in late_x:
+                    quantise_x(t)
             if ahead < TILES:
                 quantise_x(ahead)
-            late_frame = EARLY_FRAMES + step // 2
-            if late_frame < FRAMES:
-                fill_frame_table(("cos", "sin")[step % 2], late_frame)

@@ -243,7 +243,8 @@ def tile_causalwanselfattention_pa_kernel(
                         xt[:, c, u, :], x_words[:, 256 * c + u : 256 * (c + 1) : 2], ident[:]
                     )
             grouped[t] = quant.tile([P, PASSES * 4 * P], BF16, name="grouped", align_bytes=64)
-            nc.scalar.copy(
+            copy = nc.vector.tensor_copy if t > X_LEAD and t % 2 == 0 else nc.scalar.copy
+            copy(
                 out=grouped[t][:].bitcast(F32).rearrange("p (c r u) -> p c r u", c=PASSES, u=2),
                 in_=xt[:].rearrange("p c u r -> p c r u"),
             )

@@ -47,6 +47,8 @@ ACC_BANKS = (2, 3)
 Y_BANKS = (4, 5, 6, 7)
 FIRST_X_BANKS = (0, 1, 4, 5)
 FIRST_ACC_BANKS = (2, 3, 6, 7, 4, 5)
+LATE_TILE = 8
+LATE_Y_BANKS = Y_BANKS + X_BANKS
 
 FLOPS = 2 * TOKENS * K * FEATURES
 
@@ -283,7 +285,11 @@ def tile_causalwanselfattention_pa_kernel(
 
         def back(t, k):
             blk, i = divmod(t, BLOCK_TILES)
-            y_ps[t, k] = bank_tile(Y_BANKS[BANKS * (t % 2) + k], [P, BANK_HEADS, HEAD], "y_ps")
+            if t < LATE_TILE:
+                bank = Y_BANKS[BANKS * (t % 2) + k]
+            else:
+                bank = LATE_Y_BANKS[BANKS * ((t - LATE_TILE) % 3) + k]
+            y_ps[t, k] = bank_tile(bank, [P, BANK_HEADS, HEAD], "y_ps")
             for hk in range(BANK_HEADS):
                 nc.tensor.transpose(
                     y_ps[t, k][:, hk, :], y_feat[blk][:, k * BANK_HEADS + hk, i * P : (i + 1) * P], ident[:]
@@ -345,14 +351,14 @@ def tile_causalwanselfattention_pa_kernel(
                 )
                 nc.sync.dma_start(out=out_rows[t * P : (t + 1) * P, cols], in_=rotated[:, cols])
 
-        for t in range(BLOCK_TILES):
+        for t in range(BLOCK_TILES + 1):
             transpose_x(t)
             if t == 1:
                 turn_bias()
             quantise_x(t)
         fill_signed_gain()
         fill_grid_tables(0)
-        early_x = ((4, 5), (6, 7))
+        early_x = ((5, 6), (7,))
         late_x = (8,)
         early_frames = ((1, 2), (3,))
         for stage in range(2):

@@ -79,12 +79,12 @@ def tile_causalwanselfattention_pa_kernel(
         def load_x(t):
             nc.sync.dma_start(out=x_tiles[t][:], in_=x_rows[t * P : (t + 1) * P, :])
 
-        def load_angles(rows, kind):
+        def load_angles(rows, kind, queue):
             pair = {}
             for name, table in (("cos", freqs_cos), ("sin", freqs_sin)):
                 src = rows(table)
                 pair[name] = const.tile([P, src.shape[-1]], BF16, name="%s_%s" % (name, kind))
-                nc.gpsimd.dma_start(out=pair[name][:], in_=src)
+                queue.dma_start(out=pair[name][:], in_=src)
             return pair
 
         g_few = const.tile([FRAMES, FEATURES], BF16, name="g_few")
@@ -103,6 +103,7 @@ def tile_causalwanselfattention_pa_kernel(
             nc.sync.dma_start(
                 out=w_scales[r:P:32, :, :].bitcast(I32), in_=scale_rows[r].bitcast(I32)
             )
+        g_all = const.tile([P, FEATURES], BF16, name="g_all")
         words_src = W_words.rearrange("c p n -> p c n")
         piece = 2 * HEAD * STEP_HEADS
         for i in range(BLOCK_TILES):
@@ -112,6 +113,12 @@ def tile_causalwanselfattention_pa_kernel(
             )
             if i > 0:
                 load_x(BLOCK_TILES + i)
+            if i == 1:
+                nc.sync.dma_start(out=g_all[:], in_=g.partition_broadcast(P))
+            if i == BLOCK_TILES - 1:
+                by_frame = load_angles(
+                    lambda tab: tab[0:EARLY_FRAMES, :].rearrange("f j -> (f j)").partition_broadcast(P), "frame", nc.sync
+                )
         for t in range(2 * BLOCK_TILES, TILES):
             load_x(t)
         nc.sync.dma_start(out=g_few[:], in_=g.partition_broadcast(FRAMES))
@@ -119,18 +126,13 @@ def tile_causalwanselfattention_pa_kernel(
         nc.sync.dma_start(out=frame_rows["sin"][:], in_=freqs_sin[0:FRAMES, :])
         ident = const.tile([P, P], F32, name="ident")
         make_identity(nc, ident[:])
-        g_all = const.tile([P, FEATURES], BF16, name="g_all")
-        nc.gpsimd.dma_start(out=g_all[:], in_=g.partition_broadcast(P))
-        by_col = load_angles(lambda tab: tab.unsqueeze(0).to_broadcast([8, 16, TABLE_PAIRS]), "col")
+        by_col = load_angles(lambda tab: tab.unsqueeze(0).to_broadcast([8, 16, TABLE_PAIRS]), "col", nc.gpsimd)
         by_row = {}
         by_row[0] = load_angles(
-            lambda tab: tab[0:8, :].unsqueeze(1).to_broadcast([8, 16, TABLE_PAIRS]), "row0"
-        )
-        by_frame = load_angles(
-            lambda tab: tab[0:EARLY_FRAMES, :].rearrange("f j -> (f j)").partition_broadcast(P), "frame"
+            lambda tab: tab[0:8, :].unsqueeze(1).to_broadcast([8, 16, TABLE_PAIRS]), "row0", nc.gpsimd
         )
         by_row[1] = load_angles(
-            lambda tab: tab[8:16, :].unsqueeze(1).to_broadcast([8, 16, TABLE_PAIRS]), "row1"
+            lambda tab: tab[8:16, :].unsqueeze(1).to_broadcast([8, 16, TABLE_PAIRS]), "row1", nc.gpsimd
         )
         eps_col = const.tile([P, 1], F32, name="eps_col")
         nc.vector.memset(eps_col[:], EPS)

@@ -40,13 +40,16 @@ STEP_HEADS = HEADS // BLOCK_TILES
 X_LEAD = 2 * BLOCK_TILES + 1
 MX_LEAD = BLOCK_TILES
 ADDS_LAST = 2
-EARLY_FRAMES = 4
+TABLE_ROWS = 16
+VECTOR_X = (10, 12, 14)
+VECTOR_HEADS = (7,)
+EARLY_FRAMES = 1
 
 X_BANKS = (0, 1)
 ACC_BANKS = (2, 3)
 Y_BANKS = (4, 5, 6, 7)
 FIRST_X_BANKS = (0, 1, 4, 5)
-FIRST_ACC_BANKS = (2, 3, 6, 7, 4, 5)
+FIRST_ACC_BANKS = (2, 3, 6, 7)
 LATE_TILE = 8
 LATE_Y_BANKS = Y_BANKS + X_BANKS
 
@@ -74,66 +77,44 @@ def tile_causalwanselfattention_pa_kernel(
             return psum.tile(shape, F32, name="%s_%d" % (label, len(made)), offset=bank * BANK_BYTES)
 
         ctx.enter_context(tc.manual_schedule())
-        x_tiles = [const.tile([P, K], BF16, name="x%d" % t) for t in range(TILES)]
+        x_all = const.tile([P, TILES, K], BF16, name="x_all")
+        x_src = x_rows.rearrange("(t p) k -> p t k", p=P)
 
-        def load_x(t):
-            nc.sync.dma_start(out=x_tiles[t][:], in_=x_rows[t * P : (t + 1) * P, :])
+        def load_x(first, last):
+            nc.sync.dma_start(out=x_all[:, first:last, :], in_=x_src[:, first:last, :])
 
-        def load_angles(rows, kind, queue):
-            pair = {}
-            for name, table in (("cos", freqs_cos), ("sin", freqs_sin)):
-                src = rows(table)
-                pair[name] = const.tile([P, src.shape[-1]], BF16, name="%s_%s" % (name, kind))
-                queue.dma_start(out=pair[name][:], in_=src)
-            return pair
-
-        g_few = const.tile([FRAMES, FEATURES], BF16, name="g_few")
-        frame_rows = {name: const.tile([FRAMES, TABLE_PAIRS], BF16, name=name + "_frame_rows") for name in ("cos", "sin")}
-        b_rows = const.tile([P, P], BF16, name="b_rows")
-        nc.vector.memset(b_rows[:], 0.0)
-        load_x(0)
-        nc.sync.dma_start(out=b_rows[0:HEADS, :], in_=b.rearrange("(h d) -> h d", d=HEAD))
-        for t in range(1, BLOCK_TILES + 1):
-            load_x(t)
-        w_words = const.tile([P, PASSES, 2 * FEATURES], U8, name="w_words", align_bytes=64)
         w_scales = const.tile([P, PASSES, FEATURES], U8, name="w_scales", align_bytes=64)
         nc.vector.memset(w_scales[:].bitcast(I32), 0)
+        b_rows = const.tile([P, P], BF16, name="b_rows")
+        nc.vector.memset(b_rows[:], 0.0)
+        sign = const.tile([P, 2, 2], F32, name="sign")
+        nc.vector.memset(sign[:], 1.0)
+        nc.vector.memset(sign[:, 1, 1:2], -1.0)
+        g_all = const.tile([P, FEATURES], BF16, name="g_all")
+        load_x(0, 1)
+        nc.sync.dma_start(out=b_rows[0:HEADS, :], in_=b.rearrange("(h d) -> h d", d=HEAD))
+        for t in range(1, BLOCK_TILES + 1):
+            load_x(t, t + 1)
+        freq = {name: const.tile([TABLE_ROWS, TABLE_PAIRS], BF16, name=name + "_rows") for name in ("cos", "sin")}
         scale_rows = W_scales.rearrange("c (q r) n -> r q c n", r=4)
         for r in range(4):
             nc.sync.dma_start(
                 out=w_scales[r:P:32, :, :].bitcast(I32), in_=scale_rows[r].bitcast(I32)
             )
-        g_all = const.tile([P, FEATURES], BF16, name="g_all")
+        w_words = const.tile([P, PASSES, 2 * FEATURES], U8, name="w_words", align_bytes=64)
         words_src = W_words.rearrange("c p n -> p c n")
-        piece = 2 * HEAD * STEP_HEADS
-        for i in range(BLOCK_TILES):
-            nc.sync.dma_start(
-                out=w_words[:, :, i * piece : (i + 1) * piece].bitcast(I32),
-                in_=words_src[:, :, i * piece : (i + 1) * piece].bitcast(I32),
-            )
-            if i > 0:
-                load_x(BLOCK_TILES + i)
-            if i == 1:
+        for k in range(BANKS):
+            cols = slice(2 * BANK * k, 2 * BANK * (k + 1))
+            nc.sync.dma_start(out=w_words[:, :, cols].bitcast(I32), in_=words_src[:, :, cols].bitcast(I32))
+            if k == 0:
                 nc.sync.dma_start(out=g_all[:], in_=g.partition_broadcast(P))
-            if i == BLOCK_TILES - 1:
-                by_frame = load_angles(
-                    lambda tab: tab[0:EARLY_FRAMES, :].rearrange("f j -> (f j)").partition_broadcast(P), "frame", nc.sync
-                )
-        for t in range(2 * BLOCK_TILES, TILES):
-            load_x(t)
-        nc.sync.dma_start(out=g_few[:], in_=g.partition_broadcast(FRAMES))
-        nc.sync.dma_start(out=frame_rows["cos"][:], in_=freqs_cos[0:FRAMES, :])
-        nc.sync.dma_start(out=frame_rows["sin"][:], in_=freqs_sin[0:FRAMES, :])
+        load_x(5, 6)
+        for t in range(6, TILES, 2):
+            load_x(t, t + 2)
         ident = const.tile([P, P], F32, name="ident")
         make_identity(nc, ident[:])
-        by_col = load_angles(lambda tab: tab.unsqueeze(0).to_broadcast([8, 16, TABLE_PAIRS]), "col", nc.gpsimd)
-        by_row = {}
-        by_row[0] = load_angles(
-            lambda tab: tab[0:8, :].unsqueeze(1).to_broadcast([8, 16, TABLE_PAIRS]), "row0", nc.gpsimd
-        )
-        by_row[1] = load_angles(
-            lambda tab: tab[8:16, :].unsqueeze(1).to_broadcast([8, 16, TABLE_PAIRS]), "row1", nc.gpsimd
-        )
+        nc.gpsimd.dma_start(out=freq["cos"][:], in_=freqs_cos)
+        nc.gpsimd.dma_start(out=freq["sin"][:], in_=freqs_sin)
         eps_col = const.tile([P, 1], F32, name="eps_col")
         nc.vector.memset(eps_col[:], EPS)
         warm = const.tile([P, 1], F32, name="warm")
@@ -144,94 +125,84 @@ def tile_causalwanselfattention_pa_kernel(
         b_col = const.tile([P, HEADS], F32, name="b_col")
 
         def turn_bias():
-            b_ps = bank_tile(7, [P, P], "b_ps")
+            b_ps = bank_tile(6, [P, P], "b_ps")
             nc.tensor.transpose(b_ps[:], b_rows32[:], ident[:])
             nc.vector.tensor_copy(out=b_col[:], in_=b_ps[:, 0:HEADS])
 
 
-        sign = const.tile([P, 2], F32, name="sign")
-        nc.vector.memset(sign[:, 0:1], 1.0)
-        nc.vector.memset(sign[:, 1:2], -1.0)
-        g_signed = const.tile([P, FEATURES], F32, name="g_signed")
+        row_end = FRAME_PAIRS + GRID_PAIRS
+        GRID_COLS = 2 * GRID_PAIRS
+        angle_rows = const.tile([P, 2, HEAD], BF16, name="angle_rows")
+        nc.gpsimd.memset(angle_rows[:], 0.0)
+        for n, name in enumerate(("cos", "sin")):
+            nc.gpsimd.tensor_tensor(
+                out=angle_rows[0:TABLE_ROWS, n, :].rearrange("p (j i) -> p j i", i=2),
+                in0=freq[name][:].unsqueeze(2).to_broadcast([TABLE_ROWS, TABLE_PAIRS, 2]),
+                in1=sign[0:TABLE_ROWS, n, :].unsqueeze(1).to_broadcast([TABLE_ROWS, TABLE_PAIRS, 2]),
+                op=ALU.mult,
+            )
+        pick = const.tile([P, 4, P], BF16, name="pick")
+        grid = [P, 8, 16]
+        for n, src in enumerate((
+            ident[:, 0:8].unsqueeze(2).to_broadcast(grid),
+            ident[:, 8:16].unsqueeze(2).to_broadcast(grid),
+            ident[:, 0:16].unsqueeze(1).to_broadcast(grid),
+            ident[:, 0:1].unsqueeze(2).to_broadcast(grid),
+        )):
+            nc.vector.tensor_copy(out=pick[:, n, :].rearrange("p (r c) -> p r c", c=16), in_=src)
+        ROWS0, ROWS1, COLS, FIRST = 0, 2 * GRID_COLS, 4 * GRID_COLS, 6 * GRID_COLS
+        angles = const.tile([P, 6 * GRID_COLS + 2 * F_COLS], F32, name="angles")
 
-        def fill_signed_gain():
+        def pick_angles():
+            picked = bank_tile(7, [P, 6 * GRID_COLS + 2 * F_COLS], "picked")
+            for n, dst, first, last in (
+                (0, ROWS0, F_COLS, 2 * row_end),
+                (1, ROWS1, F_COLS, 2 * row_end),
+                (2, COLS, 2 * row_end, HEAD),
+                (3, FIRST, 0, F_COLS),
+            ):
+                nc.tensor.matmul(
+                    picked[:, dst : dst + 2 * (last - first)], lhsT=pick[:, n, :], rhs=angle_rows[:, :, first:last],
+                    start=True, stop=True,
+                )
+            nc.scalar.copy(out=angles[:], in_=picked[:])
+
+        def fill_table(dst, first, src, parts):
+            cols = dst.shape[-1]
             nc.vector.tensor_tensor(
-                out=g_signed[:].rearrange("p (j i) -> p j i", i=2),
-                in0=g_all[:].rearrange("p (j i) -> p j i", i=2),
-                in1=sign[:].unsqueeze(1).to_broadcast([P, FEATURES // 2, 2]),
+                out=dst,
+                in0=g_all[0:parts, :].rearrange("p (h d) -> p h d", d=HEAD)[:, :, first : first + cols]
+                .unsqueeze(1).to_broadcast([parts, 2, HEADS, cols]),
+                in1=src.unsqueeze(2).to_broadcast([parts, 2, HEADS, cols]),
                 op=ALU.mult,
             )
 
-        gain = {
-            "cos": g_all[:].rearrange("p (h d) -> p h d", d=HEAD),
-            "sin": g_signed[:].rearrange("p (h d) -> p h d", d=HEAD),
-        }
-        tab_rc = {}
-        tab_f = {}
-        for name in ("cos", "sin"):
-            tab_rc[name] = const.tile([P, 2, HEADS, RC_COLS], F32, name=name + "_tab_rc")
-        row_end = FRAME_PAIRS + GRID_PAIRS
+        tab_grid = const.tile([P, 2, 2, HEADS, RC_COLS], F32, name="tab_grid")
+        tab_frames = const.tile([P, FRAMES, 2, HEADS, F_COLS], F32, name="tab_frames")
         FRAME_TABLE = 2 * HEADS * F_COLS
         few = const.tile([FRAMES, 2, HEADS, F_COLS], F32, name="few")
-        tab_frames = const.tile([P, FRAMES, 2, HEADS, F_COLS], F32, name="tab_frames")
-        for n, name in enumerate(("cos", "sin")):
-            tab_f[name] = tab_frames[:, :, n, :, :]
         parked = out_rows[TOKENS - FRAMES : TOKENS, 0:FRAME_TABLE]
 
         def park_frame_tables():
-            for n, name in enumerate(("cos", "sin")):
-                angles = frame_rows[name][:, 0:FRAME_PAIRS].unsqueeze(2).to_broadcast([FRAMES, FRAME_PAIRS, 2])
-                if name == "sin":
-                    signed = const.tile([FRAMES, FRAME_PAIRS, 2], F32, name="signed_few")
-                    nc.vector.tensor_tensor(
-                        out=signed[:], in0=angles,
-                        in1=sign[0:FRAMES, :].unsqueeze(1).to_broadcast([FRAMES, FRAME_PAIRS, 2]), op=ALU.mult,
-                    )
-                    angles = signed[:]
-                nc.vector.tensor_tensor(
-                    out=few[:, n, :, :].rearrange("p h (j i) -> p h j i", i=2),
-                    in0=g_few[:].rearrange("p (h d) -> p h d", d=HEAD)[:, :, 0:F_COLS].rearrange("p h (j i) -> p h j i", i=2),
-                    in1=angles.unsqueeze(1).to_broadcast([FRAMES, HEADS, FRAME_PAIRS, 2]),
-                    op=ALU.mult,
-                )
+            fill_table(few[:], 0, angle_rows[0:FRAMES, :, 0:F_COLS], FRAMES)
             nc.sync.dma_start(out=parked, in_=few[:].rearrange("p n h d -> p (n h d)"))
+
+        def fetch_frame_tables(first, last):
             nc.sync.dma_start(
-                out=tab_frames[:, EARLY_FRAMES:FRAMES, :, :, :].rearrange("p f n h d -> p f (n h d)"),
-                in_=parked[EARLY_FRAMES:FRAMES, :].unsqueeze(0).to_broadcast([P, FRAMES - EARLY_FRAMES, FRAME_TABLE]),
+                out=tab_frames[:, first:last, :, :, :].rearrange("p f n h d -> p f (n h d)"),
+                in_=parked[first:last, :].unsqueeze(0).to_broadcast([P, last - first, FRAME_TABLE]),
             )
 
-
-        def fill_table(dst, gain_cols, angles, pairs, engine=nc.vector):
-            engine.tensor_tensor(
-                out=dst.rearrange("p h (j i) -> p h j i", i=2),
-                in0=gain_cols.rearrange("p h (j i) -> p h j i", i=2),
-                in1=angles.unsqueeze(1).unsqueeze(3).to_broadcast([P, HEADS, pairs, 2]),
-                op=ALU.mult,
-            )
+        def picked_angles(first, cols):
+            return angles[:, first : first + 2 * cols].rearrange("p (n d) -> p n d", n=2)
 
         def fill_grid_tables(half):
-            for name in ("cos", "sin"):
-                fill_table(
-                    tab_rc[name][:, half, :, 0 : 2 * GRID_PAIRS],
-                    gain[name][:, :, F_COLS : 2 * row_end],
-                    by_row[half][name][:, FRAME_PAIRS:row_end],
-                    GRID_PAIRS,
-                )
-                fill_table(
-                    tab_rc[name][:, half, :, 2 * GRID_PAIRS : RC_COLS],
-                    gain[name][:, :, 2 * row_end : HEAD],
-                    by_col[name][:, row_end:TABLE_PAIRS],
-                    GRID_PAIRS,
-                )
+            rows = (ROWS0, ROWS1)[half]
+            fill_table(tab_grid[:, half, :, :, 0:GRID_COLS], F_COLS, picked_angles(rows, GRID_COLS), P)
+            fill_table(tab_grid[:, half, :, :, GRID_COLS:RC_COLS], 2 * row_end, picked_angles(COLS, GRID_COLS), P)
 
-        def fill_frame_table(name, f, engine=nc.vector):
-            fill_table(
-                tab_f[name][:, f, :, :],
-                gain[name][:, :, 0:F_COLS],
-                by_frame[name][:, f * TABLE_PAIRS : f * TABLE_PAIRS + FRAME_PAIRS],
-                FRAME_PAIRS,
-                engine,
-            )
+        def fill_first_frame():
+            fill_table(tab_frames[:, 0, :, :, :], 0, picked_angles(FIRST, F_COLS), P)
 
         grouped = {}
         codes = [const.tile([P, PASSES, BLOCK], U32, name="codes%d" % blk, align_bytes=64) for blk in range(BLOCKS)]
@@ -239,7 +210,7 @@ def tile_causalwanselfattention_pa_kernel(
         y_feat = {}
 
         def transpose_x(t):
-            x_words = x_tiles[t][:].bitcast(F32)
+            x_words = x_all[:, t, :].bitcast(F32)
             xt = bank_tile(FIRST_X_BANKS[t] if t < len(FIRST_X_BANKS) else X_BANKS[t % len(X_BANKS)], [P, PASSES, 2, P], "xt")
             for c in range(PASSES):
                 for u in range(2):
@@ -247,7 +218,7 @@ def tile_causalwanselfattention_pa_kernel(
                         xt[:, c, u, :], x_words[:, 256 * c + u : 256 * (c + 1) : 2], ident[:]
                     )
             grouped[t] = quant.tile([P, PASSES * 4 * P], BF16, name="grouped", align_bytes=64)
-            copy = nc.vector.tensor_copy if t > X_LEAD and t % 2 == 0 else nc.scalar.copy
+            copy = nc.vector.tensor_copy if t in VECTOR_X else nc.scalar.copy
             copy(
                 out=grouped[t][:].bitcast(F32).rearrange("p (c r u) -> p c r u", c=PASSES, u=2),
                 in_=xt[:].rearrange("p c u r -> p c r u"),
@@ -277,9 +248,14 @@ def tile_causalwanselfattention_pa_kernel(
                     start=(c == 0),
                     stop=(c == PASSES - 1),
                 )
-            nc.scalar.activation(
-                out=y_feat[blk][:, h, :], in_=acc[:], func=ACT.Identity, bias=b_col[:, h : h + 1], scale=1.0
-            )
+            if blk == 0 and h in VECTOR_HEADS:
+                nc.vector.tensor_scalar(
+                    out=y_feat[blk][:, h, :], in0=acc[:], scalar1=b_col[:, h : h + 1], scalar2=None, op0=ALU.add
+                )
+            else:
+                nc.scalar.activation(
+                    out=y_feat[blk][:, h, :], in_=acc[:], func=ACT.Identity, bias=b_col[:, h : h + 1], scale=1.0
+                )
 
         y_ps = {}
         sums = {}
@@ -323,12 +299,12 @@ def tile_causalwanselfattention_pa_kernel(
             prod = {name: work.tile([P, HEADS, HEAD], F32, name=name + "_prod") for name in ("cos", "sin")}
             for k in range(BANKS):
                 heads = slice(k * BANK_HEADS, (k + 1) * BANK_HEADS)
-                for name in ("cos", "sin"):
+                for n, name in enumerate(("cos", "sin")):
                     nc.vector.scalar_tensor_tensor(
                         out=prod[name][:, heads, 0:F_COLS],
                         in0=y_ps[t, k][:, :, 0:F_COLS],
                         scalar=inv[t][:, 0:1],
-                        in1=tab_f[name][:, frame, heads, :],
+                        in1=tab_frames[:, frame, n, heads, :],
                         op0=ALU.mult,
                         op1=ALU.mult,
                     )
@@ -336,7 +312,7 @@ def tile_causalwanselfattention_pa_kernel(
                         out=prod[name][:, heads, F_COLS:HEAD],
                         in0=y_ps[t, k][:, :, F_COLS:HEAD],
                         scalar=inv[t][:, 0:1],
-                        in1=tab_rc[name][:, half, heads, :],
+                        in1=tab_grid[:, half, n, heads, :],
                         op0=ALU.mult,
                         op1=ALU.mult,
                     )
@@ -358,46 +334,47 @@ def tile_causalwanselfattention_pa_kernel(
             if t == 1:
                 turn_bias()
             quantise_x(t)
-        fill_signed_gain()
+        pick_angles()
         fill_grid_tables(0)
-        early_x = ((5, 6), (7,))
-        late_x = (8,)
-        early_frames = ((1, 2), (3,))
-        for stage in range(2):
-            for h in range(BANK_HEADS * stage, BANK_HEADS * (stage + 1)):
-                project(0, h)
-            for t in early_x[stage]:
-                transpose_x(t)
-            if stage == 0:
-                fill_frame_table("cos", 0)
-                fill_frame_table("sin", 0)
-                fill_grid_tables(1)
-            for t in early_x[stage]:
-                quantise_x(t)
-            for f in early_frames[stage]:
-                fill_frame_table("cos", f)
-                fill_frame_table("sin", f)
-            if stage == 1:
-                park_frame_tables()
+        project(0, 0)
+        project(0, 1)
+        fill_first_frame()
+        project(0, 2)
+        project(0, 3)
+        park_frame_tables()
+        fetch_frame_tables(EARLY_FRAMES, FRAMES // 2)
+        fetch_frame_tables(FRAMES // 2, FRAMES)
+        transpose_x(5)
+        transpose_x(6)
+        fill_grid_tables(1)
+        quantise_x(5)
+        quantise_x(6)
+        for h in range(4, 8):
+            project(0, h)
+        transpose_x(7)
+        quantise_x(7)
+        back(0, 0)
+        back(0, 1)
         for step in range(TILES):
             ahead = step + X_LEAD
             blk, i = divmod(step + MX_LEAD, BLOCK_TILES)
-            back(step, 0)
-            back(step, 1)
+            if step > 0:
+                back(step, 0)
+                back(step, 1)
             norm_first(step)
             if ahead < TILES and step > 0:
                 transpose_x(ahead)
             norm(step)
             if step == 0:
-                for t in late_x:
-                    transpose_x(t)
-                transpose_x(ahead)
+                transpose_x(8)
+                transpose_x(9)
+                pass
             if blk < BLOCKS:
-                for n in range(STEP_HEADS):
-                    project(blk, STEP_HEADS * i + n)
+                for h in range(STEP_HEADS * i, STEP_HEADS * (i + 1)):
+                    project(blk, h)
             rotate(step)
             if step == 0:
-                for t in late_x:
-                    quantise_x(t)
-            if ahead < TILES:
+                quantise_x(8)
+                quantise_x(9)
+            elif ahead < TILES:
                 quantise_x(ahead)

@@ -27,19 +27,20 @@ FRAME_PAIRS = 22
 GRID_PAIRS = 21
 TABLE_PAIRS = 64
 F_COLS = 2 * FRAME_PAIRS
+F_END = HEADS * F_COLS
 RC_COLS = HEAD - F_COLS
 BANK = 512
 BANK_BYTES = 4 * BANK
 BANK_HEADS = BANK // HEAD
 BANKS = FEATURES // BANK
 EPS = 1e-6
+FEATURE_RANGES = ((0, F_COLS, 0), (F_COLS, RC_COLS, HEADS * F_COLS))
 BLOCK_TILES = 4
 BLOCK = BLOCK_TILES * P
 BLOCKS = TILES // BLOCK_TILES
 STEP_HEADS = HEADS // BLOCK_TILES
 X_LEAD = 2 * BLOCK_TILES + 1
 MX_LEAD = BLOCK_TILES
-ADDS_LAST = 2
 TABLE_ROWS = 16
 VECTOR_X = (10, 12, 14)
 VECTOR_HEADS = (7,)
@@ -85,55 +86,73 @@ def tile_causalwanselfattention_pa_kernel(
 
         w_scales = const.tile([P, PASSES, FEATURES], U8, name="w_scales", align_bytes=64)
         nc.vector.memset(w_scales[:].bitcast(I32), 0)
-        b_rows = const.tile([P, P], BF16, name="b_rows")
-        nc.vector.memset(b_rows[:], 0.0)
+        b_row = const.tile([P, FEATURES], BF16, name="b_row")
+        nc.vector.memset(b_row[:].bitcast(U32), 0)
+        ones = const.tile([P, 2], BF16, name="ones")
+        nc.vector.memset(ones[:], 1.0)
         sign = const.tile([P, 2, 2], F32, name="sign")
         nc.vector.memset(sign[:], 1.0)
         nc.vector.memset(sign[:, 1, 1:2], -1.0)
         g_all = const.tile([P, FEATURES], BF16, name="g_all")
         load_x(0, 1)
-        nc.sync.dma_start(out=b_rows[0:HEADS, :], in_=b.rearrange("(h d) -> h d", d=HEAD))
-        for t in range(1, BLOCK_TILES + 1):
-            load_x(t, t + 1)
+        b_natural = const.tile([1, FEATURES], BF16, name="b_natural")
+        nc.sync.dma_start(out=b_natural[:], in_=b.rearrange("(o d) -> o d", o=1))
         freq = {name: const.tile([TABLE_ROWS, TABLE_PAIRS], BF16, name=name + "_rows") for name in ("cos", "sin")}
+        nc.sync.dma_start(out=freq["cos"][:], in_=freqs_cos)
+        nc.sync.dma_start(out=freq["sin"][:], in_=freqs_sin)
+        for t in range(1, BLOCK_TILES):
+            load_x(t, t + 1)
         scale_rows = W_scales.rearrange("c (q r) n -> r q c n", r=4)
         for r in range(4):
             nc.sync.dma_start(
                 out=w_scales[r:P:32, :, :].bitcast(I32), in_=scale_rows[r].bitcast(I32)
             )
         w_words = const.tile([P, PASSES, 2 * FEATURES], U8, name="w_words", align_bytes=64)
-        words_src = W_words.rearrange("c p n -> p c n")
-        for k in range(BANKS):
-            cols = slice(2 * BANK * k, 2 * BANK * (k + 1))
-            nc.sync.dma_start(out=w_words[:, :, cols].bitcast(I32), in_=words_src[:, :, cols].bitcast(I32))
-            if k == 0:
-                nc.sync.dma_start(out=g_all[:], in_=g.partition_broadcast(P))
+        load_x(4, 5)
+        nc.sync.dma_start(out=w_words[:].bitcast(I32), in_=W_words.rearrange("c p n -> p c n").bitcast(I32))
+        nc.sync.dma_start(out=g_all[:], in_=g.partition_broadcast(P))
         load_x(5, 6)
         for t in range(6, TILES, 2):
             load_x(t, t + 2)
         ident = const.tile([P, P], F32, name="ident")
         make_identity(nc, ident[:])
-        nc.gpsimd.dma_start(out=freq["cos"][:], in_=freqs_cos)
-        nc.gpsimd.dma_start(out=freq["sin"][:], in_=freqs_sin)
+        angle_rows = const.tile([P, 2, HEAD], BF16, name="angle_rows")
+        nc.gpsimd.memset(angle_rows[:], 0.0)
+        words = const.tile([P, PASSES, 2 * FEATURES], U8, name="words", align_bytes=64)
+        scales = const.tile([P, PASSES, FEATURES], U8, name="scales", align_bytes=64)
+
+        def order_weight(n):
+            first, cols, base = FEATURE_RANGES[n]
+            for dst, src, size in ((words, w_words, 2), (scales, w_scales, 1)):
+                nc.vector.tensor_copy(
+                    out=dst[:, :, size * base : size * (base + HEADS * cols)].bitcast(I32).rearrange("p c (h w) -> p c h w", h=HEADS),
+                    in_=src[:].bitcast(I32).rearrange("p c (h w) -> p c h w", h=HEADS)[:, :, :, size * first // 4 : size * (first + cols) // 4],
+                )
+
         eps_col = const.tile([P, 1], F32, name="eps_col")
         nc.vector.memset(eps_col[:], EPS)
         warm = const.tile([P, 1], F32, name="warm")
         nc.scalar.activation(out=warm[:], in_=eps_col[:], func=ACT.Abs_reciprocal_sqrt)
 
-        b_rows32 = const.tile([P, P], F32, name="b_rows32")
-        nc.vector.tensor_copy(out=b_rows32[:], in_=b_rows[:])
         b_col = const.tile([P, HEADS], F32, name="b_col")
 
-        def turn_bias():
-            b_ps = bank_tile(6, [P, P], "b_ps")
-            nc.tensor.transpose(b_ps[:], b_rows32[:], ident[:])
-            nc.vector.tensor_copy(out=b_col[:], in_=b_ps[:, 0:HEADS])
+        def order_bias():
+            for first, cols, base in FEATURE_RANGES:
+                nc.vector.tensor_copy(
+                    out=b_row[0:1, base : base + HEADS * cols].rearrange("p (h d) -> p h d", d=cols),
+                    in_=b_natural[:].rearrange("p (h d) -> p h d", d=HEAD)[:, :, first : first + cols],
+                )
 
+        def turn_bias():
+            b_ps = bank_tile(6, [P, 2 * HEADS], "b_ps")
+            for q in range(HEADS):
+                nc.tensor.matmul(
+                    b_ps[:, 2 * q : 2 * q + 2], lhsT=b_row[:, q * P : (q + 1) * P], rhs=ones[:], start=True, stop=True
+                )
+            nc.scalar.copy(out=b_col[:], in_=b_ps[:, 0 : 2 * HEADS : 2])
 
         row_end = FRAME_PAIRS + GRID_PAIRS
         GRID_COLS = 2 * GRID_PAIRS
-        angle_rows = const.tile([P, 2, HEAD], BF16, name="angle_rows")
-        nc.gpsimd.memset(angle_rows[:], 0.0)
         for n, name in enumerate(("cos", "sin")):
             nc.gpsimd.tensor_tensor(
                 out=angle_rows[0:TABLE_ROWS, n, :].rearrange("p (j i) -> p j i", i=2),
@@ -241,8 +260,8 @@ def tile_causalwanselfattention_pa_kernel(
             for c in range(PASSES):
                 nc.tensor.matmul_mx(
                     out=acc[:],
-                    lhsT=w_words[:, c, 2 * HEAD * h : 2 * HEAD * (h + 1)].bitcast(FP4X4),
-                    lhsT_scale=w_scales[:, c, HEAD * h : HEAD * (h + 1)],
+                    lhsT=words[:, c, 2 * HEAD * h : 2 * HEAD * (h + 1)].bitcast(FP4X4),
+                    lhsT_scale=scales[:, c, HEAD * h : HEAD * (h + 1)],
                     rhs=codes[blk][:, c, :].bitcast(FP8X4),
                     rhs_scale=planes[blk][:, c, :],
                     start=(c == 0),
@@ -296,51 +315,53 @@ def tile_causalwanselfattention_pa_kernel(
 
         def rotate(t):
             frame, half = divmod(t, 2)
-            prod = {name: work.tile([P, HEADS, HEAD], F32, name=name + "_prod") for name in ("cos", "sin")}
-            for k in range(BANKS):
-                heads = slice(k * BANK_HEADS, (k + 1) * BANK_HEADS)
-                for n, name in enumerate(("cos", "sin")):
-                    nc.vector.scalar_tensor_tensor(
-                        out=prod[name][:, heads, 0:F_COLS],
-                        in0=y_ps[t, k][:, :, 0:F_COLS],
-                        scalar=inv[t][:, 0:1],
-                        in1=tab_frames[:, frame, n, heads, :],
-                        op0=ALU.mult,
-                        op1=ALU.mult,
-                    )
-                    nc.vector.scalar_tensor_tensor(
-                        out=prod[name][:, heads, F_COLS:HEAD],
-                        in0=y_ps[t, k][:, :, F_COLS:HEAD],
-                        scalar=inv[t][:, 0:1],
-                        in1=tab_grid[:, half, n, heads, :],
-                        op0=ALU.mult,
-                        op1=ALU.mult,
-                    )
-            rotated = work.tile([P, FEATURES], F32, name="rotated")
-            pieces = ADDS_LAST if t == TILES - 1 else 1
-            width = FEATURES // pieces
-            for n in range(pieces):
-                cols = slice(n * width, (n + 1) * width)
+            prod = work.tile([P, 2, FEATURES], F32, name="prod")
+            f_table = tab_frames[:, frame, :, :, :].rearrange("p n h d -> p n (h d)")
+            rc_table = tab_grid[:, half, :, :, :].rearrange("p n h d -> p n (h d)")
+            for first, last, table in (
+                (0, F_END, f_table),
+                (F_END, BANK, rc_table[:, :, 0 : BANK - F_END]),
+                (BANK, FEATURES, rc_table[:, :, BANK - F_END : FEATURES - F_END]),
+            ):
+                bank, col = divmod(first, BANK)
+                nc.vector.scalar_tensor_tensor(
+                    out=prod[:, :, first:last],
+                    in0=y_ps[t, bank][:].rearrange("p h d -> p (h d)")[:, col : col + last - first]
+                    .unsqueeze(1).to_broadcast([P, 2, last - first]),
+                    scalar=inv[t][:, 0:1],
+                    in1=table,
+                    op0=ALU.mult,
+                    op1=ALU.mult,
+                )
+            rotated = work.tile([P, HEADS, HEAD], F32, name="rotated")
+            for first, cols, base in FEATURE_RANGES:
+                cos_prod, sin_prod = [
+                    prod[:, n, base : base + HEADS * cols].rearrange("p (h j i) -> p h j i", h=HEADS, i=2) for n in range(2)
+                ]
                 (nc.vector if t == TILES - 1 else nc.gpsimd).tensor_tensor(
-                    out=rotated[:, cols].rearrange("p (j i) -> p j i", i=2),
-                    in0=prod["cos"][:].rearrange("p h d -> p (h d)")[:, cols].rearrange("p (j i) -> p j i", i=2),
-                    in1=prod["sin"][:].rearrange("p h d -> p (h d)")[:, cols].rearrange("p (j i) -> p j i", i=2)[:, :, ::-1],
+                    out=rotated[:, :, first : first + cols].rearrange("p h (j i) -> p h j i", i=2),
+                    in0=cos_prod,
+                    in1=sin_prod[:, :, :, ::-1],
                     op=ALU.add,
                 )
-                nc.sync.dma_start(out=out_rows[t * P : (t + 1) * P, cols], in_=rotated[:, cols])
+            nc.sync.dma_start(out=out_rows[t * P : (t + 1) * P, :], in_=rotated[:].rearrange("p h d -> p (h d)"))
 
-        for t in range(BLOCK_TILES + 1):
+        order_bias()
+        for t in range(BLOCK_TILES):
             transpose_x(t)
-            if t == 1:
-                turn_bias()
             quantise_x(t)
         pick_angles()
-        fill_grid_tables(0)
+        transpose_x(4)
+        turn_bias()
+        order_weight(0)
         project(0, 0)
+        order_weight(1)
         project(0, 1)
-        fill_first_frame()
+        fill_grid_tables(0)
         project(0, 2)
+        fill_first_frame()
         project(0, 3)
+        quantise_x(4)
         park_frame_tables()
         fetch_frame_tables(EARLY_FRAMES, FRAMES // 2)
         fetch_frame_tables(FRAMES // 2, FRAMES)

@@ -92,7 +92,7 @@ def tile_causalwanselfattention_pa_kernel(
         nc.vector.memset(ones[:], 1.0)
         sign = const.tile([P, 2, 2], F32, name="sign")
         nc.vector.memset(sign[:], 1.0)
-        nc.vector.memset(sign[:, 1, 1:2], -1.0)
+        nc.vector.memset(sign[:, 1, 0:1], -1.0)
         g_all = const.tile([P, FEATURES], BF16, name="g_all")
         load_x(0, 1)
         b_natural = const.tile([1, FEATURES], BF16, name="b_natural")
@@ -188,13 +188,14 @@ def tile_causalwanselfattention_pa_kernel(
 
         def fill_table(dst, first, src, parts):
             cols = dst.shape[-1]
-            nc.vector.tensor_tensor(
-                out=dst,
-                in0=g_all[0:parts, :].rearrange("p (h d) -> p h d", d=HEAD)[:, :, first : first + cols]
-                .unsqueeze(1).to_broadcast([parts, 2, HEADS, cols]),
-                in1=src.unsqueeze(2).to_broadcast([parts, 2, HEADS, cols]),
-                op=ALU.mult,
-            )
+            gain = g_all[0:parts, :].rearrange("p (h j i) -> p h j i", h=HEADS, i=2)[:, :, first // 2 : (first + cols) // 2, :]
+            for n in range(2):
+                nc.vector.tensor_tensor(
+                    out=dst[:, n, :, :].rearrange("p h (j i) -> p h j i", i=2),
+                    in0=gain if n == 0 else gain[:, :, :, ::-1],
+                    in1=src[:, n, :].rearrange("p (j i) -> p j i", i=2).unsqueeze(1).to_broadcast([parts, HEADS, cols // 2, 2]),
+                    op=ALU.mult,
+                )
 
         tab_grid = const.tile([P, 2, 2, HEADS, RC_COLS], F32, name="tab_grid")
         tab_frames = const.tile([P, FRAMES, 2, HEADS, F_COLS], F32, name="tab_frames")
@@ -324,25 +325,23 @@ def tile_causalwanselfattention_pa_kernel(
                 (BANK, FEATURES, rc_table[:, :, BANK - F_END : FEATURES - F_END]),
             ):
                 bank, col = divmod(first, BANK)
-                nc.vector.scalar_tensor_tensor(
-                    out=prod[:, :, first:last],
-                    in0=y_ps[t, bank][:].rearrange("p h d -> p (h d)")[:, col : col + last - first]
-                    .unsqueeze(1).to_broadcast([P, 2, last - first]),
-                    scalar=inv[t][:, 0:1],
-                    in1=table,
-                    op0=ALU.mult,
-                    op1=ALU.mult,
-                )
+                pairs = y_ps[t, bank][:].rearrange("p h (j i) -> p (h j) i", i=2)[:, col // 2 : (col + last - first) // 2, :]
+                for n in range(2):
+                    nc.vector.scalar_tensor_tensor(
+                        out=prod[:, n, first:last].rearrange("p (j i) -> p j i", i=2),
+                        in0=pairs if n == 0 else pairs[:, :, ::-1],
+                        scalar=inv[t][:, 0:1],
+                        in1=table[:, n, :].rearrange("p (j i) -> p j i", i=2),
+                        op0=ALU.mult,
+                        op1=ALU.mult,
+                    )
             rotated = work.tile([P, HEADS, HEAD], F32, name="rotated")
             for first, cols, base in FEATURE_RANGES:
                 cos_prod, sin_prod = [
-                    prod[:, n, base : base + HEADS * cols].rearrange("p (h j i) -> p h j i", h=HEADS, i=2) for n in range(2)
+                    prod[:, n, base : base + HEADS * cols].rearrange("p (h d) -> p h d", h=HEADS) for n in range(2)
                 ]
                 (nc.vector if t == TILES - 1 else nc.gpsimd).tensor_tensor(
-                    out=rotated[:, :, first : first + cols].rearrange("p h (j i) -> p h j i", i=2),
-                    in0=cos_prod,
-                    in1=sin_prod[:, :, :, ::-1],
-                    op=ALU.add,
+                    out=rotated[:, :, first : first + cols], in0=cos_prod, in1=sin_prod, op=ALU.add
                 )
             nc.sync.dma_start(out=out_rows[t * P : (t + 1) * P, :], in_=rotated[:].rearrange("p h d -> p (h d)"))
 

@@ -114,6 +114,8 @@ def tile_causalwanselfattention_pa_kernel(
         load_x(5, 6)
         for t in range(6, TILES, 2):
             load_x(t, t + 2)
+        zeros = const.tile([P, BANK], BF16, name="zeros")
+        nc.gpsimd.memset(zeros[:].bitcast(U32), 0)
         ident = const.tile([P, P], F32, name="ident")
         make_identity(nc, ident[:])
         angle_rows = const.tile([P, 2, HEAD], BF16, name="angle_rows")
@@ -228,6 +230,11 @@ def tile_causalwanselfattention_pa_kernel(
         codes = [const.tile([P, PASSES, BLOCK], U32, name="codes%d" % blk, align_bytes=64) for blk in range(BLOCKS)]
         planes = [const.tile([P, PASSES, BLOCK], U8, name="planes%d" % blk, align_bytes=64) for blk in range(BLOCKS)]
         y_feat = {}
+        warm_bank = bank_tile(3, [P, BANK], "warm_bank")
+
+        def keep_warm(count):
+            for n in range(count):
+                nc.tensor.matmul(warm_bank[:], lhsT=zeros[:, 0:P], rhs=zeros[:], start=True, stop=True)
 
         def transpose_x(t):
             x_words = x_all[:, t, :].bitcast(F32)
@@ -336,22 +343,33 @@ def tile_causalwanselfattention_pa_kernel(
                         op1=ALU.mult,
                     )
             rotated = work.tile([P, HEADS, HEAD], F32, name="rotated")
-            for first, cols, base in FEATURE_RANGES:
-                cos_prod, sin_prod = [
-                    prod[:, n, base : base + HEADS * cols].rearrange("p (h d) -> p h d", h=HEADS) for n in range(2)
-                ]
-                (nc.vector if t == TILES - 1 else nc.gpsimd).tensor_tensor(
-                    out=rotated[:, :, first : first + cols], in0=cos_prod, in1=sin_prod, op=ALU.add
+            last_tile = t == TILES - 1
+            count = HEADS // 2 if last_tile else HEADS
+            for head in range(0, HEADS, count):
+                for first, cols, base in FEATURE_RANGES:
+                    cos_prod, sin_prod = [
+                        prod[:, n, base + head * cols : base + (head + count) * cols].rearrange("p (h d) -> p h d", h=count)
+                        for n in range(2)
+                    ]
+                    (nc.vector if last_tile else nc.gpsimd).tensor_tensor(
+                        out=rotated[:, head : head + count, first : first + cols], in0=cos_prod, in1=sin_prod, op=ALU.add
+                    )
+                nc.sync.dma_start(
+                    out=out_rows[t * P : (t + 1) * P, head * HEAD : (head + count) * HEAD],
+                    in_=rotated[:, head : head + count, :].rearrange("p h d -> p (h d)"),
                 )
-            nc.sync.dma_start(out=out_rows[t * P : (t + 1) * P, :], in_=rotated[:].rearrange("p h d -> p (h d)"))
 
         order_bias()
+        keep_warm(4)
         for t in range(BLOCK_TILES):
             transpose_x(t)
+            if t % 2 == 1:
+                keep_warm(1)
             quantise_x(t)
         pick_angles()
         transpose_x(4)
         turn_bias()
+        keep_warm(2)
         order_weight(0)
         project(0, 0)
         order_weight(1)

@@ -42,8 +42,8 @@ STEP_HEADS = HEADS // BLOCK_TILES
 X_LEAD = 2 * BLOCK_TILES + 1
 MX_LEAD = BLOCK_TILES
 TABLE_ROWS = 16
-VECTOR_X = (10, 12, 14)
-VECTOR_HEADS = (7,)
+VECTOR_X = (8, 10, 12, 14)
+VECTOR_BIAS = ((0, 7), (2, 7), (3, 3), (3, 7))
 EARLY_FRAMES = 1
 
 X_BANKS = (0, 1)
@@ -275,7 +275,7 @@ def tile_causalwanselfattention_pa_kernel(
                     start=(c == 0),
                     stop=(c == PASSES - 1),
                 )
-            if blk == 0 and h in VECTOR_HEADS:
+            if (blk, h) in VECTOR_BIAS:
                 nc.vector.tensor_scalar(
                     out=y_feat[blk][:, h, :], in0=acc[:], scalar1=b_col[:, h : h + 1], scalar2=None, op0=ALU.add
                 )

@@ -43,7 +43,9 @@ X_LEAD = 2 * BLOCK_TILES + 1
 MX_LEAD = BLOCK_TILES
 TABLE_ROWS = 16
 VECTOR_X = (8, 10, 12, 14)
-VECTOR_BIAS = ((0, 7), (2, 7), (3, 3), (3, 7))
+VECTOR_BIAS = ((0, 7),)
+TURN_FRAMES = BLOCK_TILES // 2
+TURN_CHUNKS = 3
 EARLY_FRAMES = 1
 
 X_BANKS = (0, 1)
@@ -51,7 +53,7 @@ ACC_BANKS = (2, 3)
 Y_BANKS = (4, 5, 6, 7)
 FIRST_X_BANKS = (0, 1, 4, 5)
 FIRST_ACC_BANKS = (2, 3, 6, 7)
-LATE_TILE = 8
+LATE_TILE = 12
 LATE_Y_BANKS = Y_BANKS + X_BANKS
 
 FLOPS = 2 * TOKENS * K * FEATURES
@@ -69,6 +71,7 @@ def tile_causalwanselfattention_pa_kernel(
         quant = ctx.enter_context(tc.tile_pool(name="quant", bufs=6))
         feat = ctx.enter_context(tc.tile_pool(name="feat", bufs=2))
         work = ctx.enter_context(tc.tile_pool(name="work", bufs=3))
+        outs = ctx.enter_context(tc.tile_pool(name="outs", bufs=5))
         small = ctx.enter_context(tc.tile_pool(name="small", bufs=4))
         psum = ctx.enter_context(tc.psum_pool(name="psum", bufs=1))
         made = []
@@ -120,16 +123,19 @@ def tile_causalwanselfattention_pa_kernel(
         make_identity(nc, ident[:])
         angle_rows = const.tile([P, 2, HEAD], BF16, name="angle_rows")
         nc.gpsimd.memset(angle_rows[:], 0.0)
-        words = const.tile([P, PASSES, 2 * FEATURES], U8, name="words", align_bytes=64)
-        scales = const.tile([P, PASSES, FEATURES], U8, name="scales", align_bytes=64)
+        words = [const.tile([P, 2 * FEATURES], U8, name="words%d" % c, align_bytes=64) for c in range(PASSES)]
+        scales = [const.tile([P, FEATURES], U8, name="scales%d" % c, align_bytes=64) for c in range(PASSES)]
 
         def order_weight(n):
             first, cols, base = FEATURE_RANGES[n]
-            for dst, src, size in ((words, w_words, 2), (scales, w_scales, 1)):
-                nc.vector.tensor_copy(
-                    out=dst[:, :, size * base : size * (base + HEADS * cols)].bitcast(I32).rearrange("p c (h w) -> p c h w", h=HEADS),
-                    in_=src[:].bitcast(I32).rearrange("p c (h w) -> p c h w", h=HEADS)[:, :, :, size * first // 4 : size * (first + cols) // 4],
-                )
+            for c in range(PASSES):
+                for dst, src, size in ((words[c], w_words, 2), (scales[c], w_scales, 1)):
+                    nc.vector.tensor_copy(
+                        out=dst[:, size * base : size * (base + HEADS * cols)].bitcast(I32).rearrange("p (h w) -> p h w", h=HEADS),
+                        in_=src[:, c, :].bitcast(I32).rearrange("p (h w) -> p h w", h=HEADS)[
+                            :, :, size * first // 4 : size * (first + cols) // 4
+                        ],
+                    )
 
         eps_col = const.tile([P, 1], F32, name="eps_col")
         nc.vector.memset(eps_col[:], EPS)
@@ -202,12 +208,22 @@ def tile_causalwanselfattention_pa_kernel(
         tab_grid = const.tile([P, 2, 2, HEADS, RC_COLS], F32, name="tab_grid")
         tab_frames = const.tile([P, FRAMES, 2, HEADS, F_COLS], F32, name="tab_frames")
         FRAME_TABLE = 2 * HEADS * F_COLS
-        few = const.tile([FRAMES, 2, HEADS, F_COLS], F32, name="few")
+        few = const.tile([P, 3, TURN_CHUNKS * P], F32, name="few")
+        nc.gpsimd.memset(few[:], 0.0)
         parked = out_rows[TOKENS - FRAMES : TOKENS, 0:FRAME_TABLE]
 
         def park_frame_tables():
-            fill_table(few[:], 0, angle_rows[0:FRAMES, :, 0:F_COLS], FRAMES)
-            nc.sync.dma_start(out=parked, in_=few[:].rearrange("p n h d -> p (n h d)"))
+            tables = few[0:FRAMES, :, 0:F_END].rearrange("p n (h d) -> p n h d", h=HEADS)
+            fill_table(tables[:, 0:2, :, :], 0, angle_rows[0:FRAMES, :, 0:F_COLS], FRAMES)
+            nc.sync.dma_start(out=parked.rearrange("f (n k) -> f n k", n=2), in_=few[0:FRAMES, 0:2, 0:F_END])
+            nc.vector.scalar_tensor_tensor(
+                out=tables[:, 2, :, :],
+                in0=g_all[0:FRAMES, :].rearrange("p (h d) -> p h d", d=HEAD)[:, :, 0:F_COLS],
+                scalar=-1.0,
+                in1=angle_rows[0:FRAMES, 1, 0:F_COLS].unsqueeze(1).to_broadcast([FRAMES, HEADS, F_COLS]),
+                op0=ALU.mult,
+                op1=ALU.mult,
+            )
 
         def fetch_frame_tables(first, last):
             nc.sync.dma_start(
@@ -225,6 +241,38 @@ def tile_causalwanselfattention_pa_kernel(
 
         def fill_first_frame():
             fill_table(tab_frames[:, 0, :, :, :], 0, picked_angles(FIRST, F_COLS), P)
+
+        turns = [const.tile([P, TURN_CHUNKS, P], F32, name="turn%d" % n) for n in range(TURN_FRAMES)]
+        diagonal = const.tile([P, TURN_CHUNKS, P], F32, name="diagonal")
+        turn_cols = const.tile([P, 2, TURN_CHUNKS, TURN_FRAMES], F32, name="turn_cols")
+        ident_ps = {}
+
+        def fetch_turn_columns():
+            for n in range(2):
+                flipped = bank_tile(X_BANKS[n], [P, TURN_CHUNKS + 1, P], "flipped")
+                for q in range(TURN_CHUNKS):
+                    nc.tensor.transpose(flipped[:, q, :], few[:, 2 * n, q * P : (q + 1) * P], ident[:])
+                if n == 0:
+                    nc.tensor.transpose(flipped[:, TURN_CHUNKS, :], ident[:], ident[:])
+                    ident_ps[0] = flipped[:, TURN_CHUNKS, :]
+                nc.vector.tensor_copy(
+                    out=turn_cols[:, n, :, :], in_=flipped[:, 0:TURN_CHUNKS, FRAMES - TURN_FRAMES : FRAMES]
+                )
+
+        def fill_turn(f):
+            for q in range(TURN_CHUNKS):
+                nc.vector.tensor_scalar(
+                    out=diagonal[:, q, :], in0=ident_ps[0], scalar1=turn_cols[:, 0, q, f : f + 1], scalar2=None, op0=ALU.mult
+                )
+            for q in range(TURN_CHUNKS):
+                nc.vector.scalar_tensor_tensor(
+                    out=turns[f][:, q, :].rearrange("p (j i) -> p j i", i=2),
+                    in0=ident_ps[0].rearrange("p (j i) -> p j i", i=2)[:, :, ::-1],
+                    scalar=turn_cols[:, 1, q, f : f + 1],
+                    in1=diagonal[:, q, :].rearrange("p (j i) -> p j i", i=2),
+                    op0=ALU.mult,
+                    op1=ALU.add,
+                )
 
         grouped = {}
         codes = [const.tile([P, PASSES, BLOCK], U32, name="codes%d" % blk, align_bytes=64) for blk in range(BLOCKS)]
@@ -268,8 +316,8 @@ def tile_causalwanselfattention_pa_kernel(
             for c in range(PASSES):
                 nc.tensor.matmul_mx(
                     out=acc[:],
-                    lhsT=words[:, c, 2 * HEAD * h : 2 * HEAD * (h + 1)].bitcast(FP4X4),
-                    lhsT_scale=scales[:, c, HEAD * h : HEAD * (h + 1)],
+                    lhsT=words[c][:, 2 * HEAD * h : 2 * HEAD * (h + 1)].bitcast(FP4X4),
+                    lhsT_scale=scales[c][:, HEAD * h : HEAD * (h + 1)],
                     rhs=codes[blk][:, c, :].bitcast(FP8X4),
                     rhs_scale=planes[blk][:, c, :],
                     start=(c == 0),
@@ -306,6 +354,18 @@ def tile_causalwanselfattention_pa_kernel(
                 out=squares[:], in_=y_ps[t, k][:], func=ACT.Square, accum_out=sums[t][:, k : k + 1]
             )
 
+        turned = {}
+
+        def turn_back(t):
+            blk, i = divmod(t, BLOCK_TILES)
+            turned[t] = bank_tile(ACC_BANKS[t % len(ACC_BANKS)], [P, F_END], "turned")
+            for q in range(TURN_CHUNKS):
+                cols = slice(q * P, min((q + 1) * P, F_END))
+                nc.tensor.matmul(
+                    turned[t][:, cols], lhsT=y_feat[blk][:, q, i * P : (i + 1) * P],
+                    rhs=turns[i // 2][:, q, 0 : cols.stop - cols.start], start=True, stop=True,
+                )
+
         part = {}
 
         def norm_first(t):
@@ -326,11 +386,18 @@ def tile_causalwanselfattention_pa_kernel(
             prod = work.tile([P, 2, FEATURES], F32, name="prod")
             f_table = tab_frames[:, frame, :, :, :].rearrange("p n h d -> p n (h d)")
             rc_table = tab_grid[:, half, :, :, :].rearrange("p n h d -> p n (h d)")
-            for first, last, table in (
+            ranges = [
                 (0, F_END, f_table),
                 (F_END, BANK, rc_table[:, :, 0 : BANK - F_END]),
                 (BANK, FEATURES, rc_table[:, :, BANK - F_END : FEATURES - F_END]),
-            ):
+            ]
+            rotated = outs.tile([P, HEADS, HEAD], F32, name="rotated")
+            if t in turned:
+                nc.scalar.activation(
+                    out=rotated[:, :, 0:F_COLS], in_=turned[t][:].rearrange("p (h d) -> p h d", h=HEADS), func=ACT.Copy,
+                    scale=inv[t][:, 0:1],
+                )
+            for first, last, table in ranges[1:] if t in turned else ranges:
                 bank, col = divmod(first, BANK)
                 pairs = y_ps[t, bank][:].rearrange("p h (j i) -> p (h j) i", i=2)[:, col // 2 : (col + last - first) // 2, :]
                 for n in range(2):
@@ -342,11 +409,10 @@ def tile_causalwanselfattention_pa_kernel(
                         op0=ALU.mult,
                         op1=ALU.mult,
                     )
-            rotated = work.tile([P, HEADS, HEAD], F32, name="rotated")
             last_tile = t == TILES - 1
             count = HEADS // 2 if last_tile else HEADS
             for head in range(0, HEADS, count):
-                for first, cols, base in FEATURE_RANGES:
+                for first, cols, base in FEATURE_RANGES[1:] if t in turned else FEATURE_RANGES:
                     cos_prod, sin_prod = [
                         prod[:, n, base + head * cols : base + (head + count) * cols].rearrange("p (h d) -> p h d", h=count)
                         for n in range(2)
@@ -381,7 +447,7 @@ def tile_causalwanselfattention_pa_kernel(
         quantise_x(4)
         park_frame_tables()
         fetch_frame_tables(EARLY_FRAMES, FRAMES // 2)
-        fetch_frame_tables(FRAMES // 2, FRAMES)
+        fetch_frame_tables(FRAMES // 2, FRAMES - TURN_FRAMES)
         transpose_x(5)
         transpose_x(6)
         fill_grid_tables(1)
@@ -399,6 +465,8 @@ def tile_causalwanselfattention_pa_kernel(
             if step > 0:
                 back(step, 0)
                 back(step, 1)
+            if step >= TILES - BLOCK_TILES:
+                turn_back(step)
             norm_first(step)
             if ahead < TILES and step > 0:
                 transpose_x(ahead)
@@ -411,6 +479,10 @@ def tile_causalwanselfattention_pa_kernel(
                 for h in range(STEP_HEADS * i, STEP_HEADS * (i + 1)):
                     project(blk, h)
             rotate(step)
+            if step == 7:
+                fetch_turn_columns()
+            if step in (8, 9):
+                fill_turn(step - 8)
             if step == 0:
                 quantise_x(8)
                 quantise_x(9)

@@ -42,8 +42,9 @@ STEP_HEADS = HEADS // BLOCK_TILES
 X_LEAD = 2 * BLOCK_TILES + 1
 MX_LEAD = BLOCK_TILES
 TABLE_ROWS = 16
-VECTOR_X = (8, 10, 12, 14)
+VECTOR_X = (7, 8, 10, 12, 14)
 VECTOR_BIAS = ((0, 7),)
+TURN_TILE = TILES - BLOCK_TILES
 TURN_FRAMES = BLOCK_TILES // 2
 TURN_CHUNKS = 3
 EARLY_FRAMES = 1
@@ -53,7 +54,7 @@ ACC_BANKS = (2, 3)
 Y_BANKS = (4, 5, 6, 7)
 FIRST_X_BANKS = (0, 1, 4, 5)
 FIRST_ACC_BANKS = (2, 3, 6, 7)
-LATE_TILE = 12
+LATE_TILE = 10
 LATE_Y_BANKS = Y_BANKS + X_BANKS
 
 FLOPS = 2 * TOKENS * K * FEATURES
@@ -355,6 +356,7 @@ def tile_causalwanselfattention_pa_kernel(
             )
 
         turned = {}
+        prods = {}
 
         def turn_back(t):
             blk, i = divmod(t, BLOCK_TILES)
@@ -391,13 +393,8 @@ def tile_causalwanselfattention_pa_kernel(
                 (F_END, BANK, rc_table[:, :, 0 : BANK - F_END]),
                 (BANK, FEATURES, rc_table[:, :, BANK - F_END : FEATURES - F_END]),
             ]
-            rotated = outs.tile([P, HEADS, HEAD], F32, name="rotated")
-            if t in turned:
-                nc.scalar.activation(
-                    out=rotated[:, :, 0:F_COLS], in_=turned[t][:].rearrange("p (h d) -> p h d", h=HEADS), func=ACT.Copy,
-                    scale=inv[t][:, 0:1],
-                )
-            for first, last, table in ranges[1:] if t in turned else ranges:
+            prods[t] = prod
+            for first, last, table in ranges[1:] if t >= TURN_TILE else ranges:
                 bank, col = divmod(first, BANK)
                 pairs = y_ps[t, bank][:].rearrange("p h (j i) -> p (h j) i", i=2)[:, col // 2 : (col + last - first) // 2, :]
                 for n in range(2):
@@ -409,10 +406,18 @@ def tile_causalwanselfattention_pa_kernel(
                         op0=ALU.mult,
                         op1=ALU.mult,
                     )
+        def finish(t):
+            prod = prods[t]
+            rotated = outs.tile([P, HEADS, HEAD], F32, name="rotated")
+            if t >= TURN_TILE:
+                nc.scalar.activation(
+                    out=rotated[:, :, 0:F_COLS], in_=turned[t][:].rearrange("p (h d) -> p h d", h=HEADS), func=ACT.Copy,
+                    scale=inv[t][:, 0:1],
+                )
             last_tile = t == TILES - 1
             count = HEADS // 2 if last_tile else HEADS
             for head in range(0, HEADS, count):
-                for first, cols, base in FEATURE_RANGES[1:] if t in turned else FEATURE_RANGES:
+                for first, cols, base in FEATURE_RANGES[1:] if t >= TURN_TILE else FEATURE_RANGES:
                     cos_prod, sin_prod = [
                         prod[:, n, base + head * cols : base + (head + count) * cols].rearrange("p (h d) -> p h d", h=count)
                         for n in range(2)
@@ -465,12 +470,13 @@ def tile_causalwanselfattention_pa_kernel(
             if step > 0:
                 back(step, 0)
                 back(step, 1)
-            if step >= TILES - BLOCK_TILES:
-                turn_back(step)
             norm_first(step)
             if ahead < TILES and step > 0:
                 transpose_x(ahead)
             norm(step)
+            if step > TURN_TILE:
+                turn_back(step - 1)
+                finish(step - 1)
             if step == 0:
                 transpose_x(8)
                 transpose_x(9)
@@ -479,6 +485,11 @@ def tile_causalwanselfattention_pa_kernel(
                 for h in range(STEP_HEADS * i, STEP_HEADS * (i + 1)):
                     project(blk, h)
             rotate(step)
+            if step < TURN_TILE:
+                finish(step)
+            if step == TILES - 1:
+                turn_back(step)
+                finish(step)
             if step == 7:
                 fetch_turn_columns()
             if step in (8, 9):

@@ -415,7 +415,7 @@ def tile_causalwanselfattention_pa_kernel(
                     scale=inv[t][:, 0:1],
                 )
             last_tile = t == TILES - 1
-            count = HEADS // 2 if last_tile else HEADS
+            count = HEADS // 2 if t >= TILES - 2 else HEADS
             for head in range(0, HEADS, count):
                 for first, cols, base in FEATURE_RANGES[1:] if t >= TURN_TILE else FEATURE_RANGES:
                     cos_prod, sin_prod = [
@@ -434,13 +434,10 @@ def tile_causalwanselfattention_pa_kernel(
         keep_warm(4)
         for t in range(BLOCK_TILES):
             transpose_x(t)
-            if t % 2 == 1:
-                keep_warm(1)
             quantise_x(t)
         pick_angles()
         transpose_x(4)
         turn_bias()
-        keep_warm(2)
         order_weight(0)
         project(0, 0)
         order_weight(1)
@@ -469,9 +466,11 @@ def tile_causalwanselfattention_pa_kernel(
             blk, i = divmod(step + MX_LEAD, BLOCK_TILES)
             if step > 0:
                 back(step, 0)
+                if i == 0 and ahead < TILES:
+                    transpose_x(ahead)
                 back(step, 1)
             norm_first(step)
-            if ahead < TILES and step > 0:
+            if ahead < TILES and i > 0:
                 transpose_x(ahead)
             norm(step)
             if step > TURN_TILE:

@@ -438,6 +438,7 @@ def tile_causalwanselfattention_pa_kernel(
         pick_angles()
         transpose_x(4)
         turn_bias()
+        keep_warm(2)
         order_weight(0)
         project(0, 0)
         order_weight(1)

from contextlib import ExitStack

import concourse.mybir as mybir
from concourse.masks import make_identity

F32 = mybir.dt.float32
BF16 = mybir.dt.bfloat16
I32 = mybir.dt.int32
U32 = mybir.dt.uint32
U8 = mybir.dt.uint8
FP8X4 = mybir.dt.float8_e4m3fn_x4
FP4X4 = mybir.dt.float4_e2m1fn_x4
ALU = mybir.AluOpType
ACT = mybir.ActivationFunctionType

P = 128
TOKENS = 2048
K = 1024
FEATURES = 1024
HEADS = 8
HEAD = 128
K_PASS = 512
PASSES = K // K_PASS
TILES = TOKENS // P
FRAMES = 8
FRAME_PAIRS = 22
GRID_PAIRS = 21
TABLE_PAIRS = 64
F_COLS = 2 * FRAME_PAIRS
F_END = HEADS * F_COLS
RC_COLS = HEAD - F_COLS
BANK = 512
BANK_BYTES = 4 * BANK
BANK_HEADS = BANK // HEAD
BANKS = FEATURES // BANK
EPS = 1e-6
FEATURE_RANGES = ((0, F_COLS, 0), (F_COLS, RC_COLS, HEADS * F_COLS))
BLOCK_TILES = 4
BLOCK = BLOCK_TILES * P
BLOCKS = TILES // BLOCK_TILES
STEP_HEADS = HEADS // BLOCK_TILES
X_LEAD = 2 * BLOCK_TILES + 1
MX_LEAD = BLOCK_TILES
TABLE_ROWS = 16
VECTOR_X = (7, 8, 10, 12, 14)
VECTOR_BIAS = ((0, 7),)
TURN_TILE = TILES - BLOCK_TILES
TURN_FRAMES = BLOCK_TILES // 2
TURN_CHUNKS = 3
EARLY_FRAMES = 1

X_BANKS = (0, 1)
ACC_BANKS = (2, 3)
Y_BANKS = (4, 5, 6, 7)
FIRST_X_BANKS = (0, 1, 4, 5)
FIRST_ACC_BANKS = (2, 3, 6, 7)
LATE_TILE = 10
LATE_Y_BANKS = Y_BANKS + X_BANKS

FLOPS = 2 * TOKENS * K * FEATURES


def tile_causalwanselfattention_pa_kernel(
    tc, x, W_words, W_scales, b, g, freqs_cos, freqs_sin, out
):
    nc = tc.nc
    x_rows = x.rearrange("o l k -> (o l) k")
    out_rows = out.rearrange("o l h d -> (o l) (h d)")

    with ExitStack() as ctx:
        const = ctx.enter_context(tc.tile_pool(name="const", bufs=1))
        quant = ctx.enter_context(tc.tile_pool(name="quant", bufs=6))
        feat = ctx.enter_context(tc.tile_pool(name="feat", bufs=2))
        work = ctx.enter_context(tc.tile_pool(name="work", bufs=3))
        outs = ctx.enter_context(tc.tile_pool(name="outs", bufs=5))
        small = ctx.enter_context(tc.tile_pool(name="small", bufs=4))
        psum = ctx.enter_context(tc.psum_pool(name="psum", bufs=1))
        made = []

        def bank_tile(bank, shape, label):
            made.append(label)
            return psum.tile(shape, F32, name="%s_%d" % (label, len(made)), offset=bank * BANK_BYTES)

        ctx.enter_context(tc.manual_schedule())
        x_all = const.tile([P, TILES, K], BF16, name="x_all")
        x_src = x_rows.rearrange("(t p) k -> p t k", p=P)

        def load_x(first, last):
            nc.sync.dma_start(out=x_all[:, first:last, :], in_=x_src[:, first:last, :])

        w_scales = const.tile([P, PASSES, FEATURES], U8, name="w_scales", align_bytes=64)
        nc.vector.memset(w_scales[:].bitcast(I32), 0)
        b_row = const.tile([P, FEATURES], BF16, name="b_row")
        nc.vector.memset(b_row[:].bitcast(U32), 0)
        ones = const.tile([P, 2], BF16, name="ones")
        nc.vector.memset(ones[:], 1.0)
        sign = const.tile([P, 2, 2], F32, name="sign")
        nc.vector.memset(sign[:], 1.0)
        nc.vector.memset(sign[:, 1, 0:1], -1.0)
        g_all = const.tile([P, FEATURES], BF16, name="g_all")
        load_x(0, 1)
        b_natural = const.tile([1, FEATURES], BF16, name="b_natural")
        nc.sync.dma_start(out=b_natural[:], in_=b.rearrange("(o d) -> o d", o=1))
        freq = {name: const.tile([TABLE_ROWS, TABLE_PAIRS], BF16, name=name + "_rows") for name in ("cos", "sin")}
        nc.sync.dma_start(out=freq["cos"][:], in_=freqs_cos)
        nc.sync.dma_start(out=freq["sin"][:], in_=freqs_sin)
        for t in range(1, BLOCK_TILES):
            load_x(t, t + 1)
        scale_rows = W_scales.rearrange("c (q r) n -> r q c n", r=4)
        for r in range(4):
            nc.sync.dma_start(
                out=w_scales[r:P:32, :, :].bitcast(I32), in_=scale_rows[r].bitcast(I32)
            )
        w_words = const.tile([P, PASSES, 2 * FEATURES], U8, name="w_words", align_bytes=64)
        load_x(4, 5)
        nc.sync.dma_start(out=w_words[:].bitcast(I32), in_=W_words.rearrange("c p n -> p c n").bitcast(I32))
        nc.sync.dma_start(out=g_all[:], in_=g.partition_broadcast(P))
        load_x(5, 6)
        for t in range(6, TILES, 2):
            load_x(t, t + 2)
        zeros = const.tile([P, BANK], BF16, name="zeros")
        nc.gpsimd.memset(zeros[:].bitcast(U32), 0)
        ident = const.tile([P, P], F32, name="ident")
        make_identity(nc, ident[:])
        angle_rows = const.tile([P, 2, HEAD], BF16, name="angle_rows")
        nc.gpsimd.memset(angle_rows[:], 0.0)
        words = [const.tile([P, 2 * FEATURES], U8, name="words%d" % c, align_bytes=64) for c in range(PASSES)]
        scales = [const.tile([P, FEATURES], U8, name="scales%d" % c, align_bytes=64) for c in range(PASSES)]

        def order_weight(n):
            first, cols, base = FEATURE_RANGES[n]
            for c in range(PASSES):
                for dst, src, size in ((words[c], w_words, 2), (scales[c], w_scales, 1)):
                    nc.vector.tensor_copy(
                        out=dst[:, size * base : size * (base + HEADS * cols)].bitcast(I32).rearrange("p (h w) -> p h w", h=HEADS),
                        in_=src[:, c, :].bitcast(I32).rearrange("p (h w) -> p h w", h=HEADS)[
                            :, :, size * first // 4 : size * (first + cols) // 4
                        ],
                    )

        eps_col = const.tile([P, 1], F32, name="eps_col")
        nc.vector.memset(eps_col[:], EPS)
        warm = const.tile([P, 1], F32, name="warm")
        nc.scalar.activation(out=warm[:], in_=eps_col[:], func=ACT.Abs_reciprocal_sqrt)

        b_col = const.tile([P, HEADS], F32, name="b_col")

        def order_bias():
            for first, cols, base in FEATURE_RANGES:
                nc.vector.tensor_copy(
                    out=b_row[0:1, base : base + HEADS * cols].rearrange("p (h d) -> p h d", d=cols),
                    in_=b_natural[:].rearrange("p (h d) -> p h d", d=HEAD)[:, :, first : first + cols],
                )

        def turn_bias():
            b_ps = bank_tile(6, [P, 2 * HEADS], "b_ps")
            for q in range(HEADS):
                nc.tensor.matmul(
                    b_ps[:, 2 * q : 2 * q + 2], lhsT=b_row[:, q * P : (q + 1) * P], rhs=ones[:], start=True, stop=True
                )
            nc.scalar.copy(out=b_col[:], in_=b_ps[:, 0 : 2 * HEADS : 2])

        row_end = FRAME_PAIRS + GRID_PAIRS
        GRID_COLS = 2 * GRID_PAIRS
        for n, name in enumerate(("cos", "sin")):
            nc.gpsimd.tensor_tensor(
                out=angle_rows[0:TABLE_ROWS, n, :].rearrange("p (j i) -> p j i", i=2),
                in0=freq[name][:].unsqueeze(2).to_broadcast([TABLE_ROWS, TABLE_PAIRS, 2]),
                in1=sign[0:TABLE_ROWS, n, :].unsqueeze(1).to_broadcast([TABLE_ROWS, TABLE_PAIRS, 2]),
                op=ALU.mult,
            )
        pick = const.tile([P, 4, P], BF16, name="pick")
        grid = [P, 8, 16]
        for n, src in enumerate((
            ident[:, 0:8].unsqueeze(2).to_broadcast(grid),
            ident[:, 8:16].unsqueeze(2).to_broadcast(grid),
            ident[:, 0:16].unsqueeze(1).to_broadcast(grid),
            ident[:, 0:1].unsqueeze(2).to_broadcast(grid),
        )):
            nc.vector.tensor_copy(out=pick[:, n, :].rearrange("p (r c) -> p r c", c=16), in_=src)
        ROWS0, ROWS1, COLS, FIRST = 0, 2 * GRID_COLS, 4 * GRID_COLS, 6 * GRID_COLS
        angles = const.tile([P, 6 * GRID_COLS + 2 * F_COLS], F32, name="angles")

        def pick_angles():
            picked = bank_tile(7, [P, 6 * GRID_COLS + 2 * F_COLS], "picked")
            for n, dst, first, last in (
                (0, ROWS0, F_COLS, 2 * row_end),
                (1, ROWS1, F_COLS, 2 * row_end),
                (2, COLS, 2 * row_end, HEAD),
                (3, FIRST, 0, F_COLS),
            ):
                nc.tensor.matmul(
                    picked[:, dst : dst + 2 * (last - first)], lhsT=pick[:, n, :], rhs=angle_rows[:, :, first:last],
                    start=True, stop=True,
                )
            nc.scalar.copy(out=angles[:], in_=picked[:])

        def fill_table(dst, first, src, parts):
            cols = dst.shape[-1]
            gain = g_all[0:parts, :].rearrange("p (h j i) -> p h j i", h=HEADS, i=2)[:, :, first // 2 : (first + cols) // 2, :]
            for n in range(2):
                nc.vector.tensor_tensor(
                    out=dst[:, n, :, :].rearrange("p h (j i) -> p h j i", i=2),
                    in0=gain if n == 0 else gain[:, :, :, ::-1],
                    in1=src[:, n, :].rearrange("p (j i) -> p j i", i=2).unsqueeze(1).to_broadcast([parts, HEADS, cols // 2, 2]),
                    op=ALU.mult,
                )

        tab_grid = const.tile([P, 2, 2, HEADS, RC_COLS], F32, name="tab_grid")
        tab_frames = const.tile([P, FRAMES, 2, HEADS, F_COLS], F32, name="tab_frames")
        FRAME_TABLE = 2 * HEADS * F_COLS
        few = const.tile([P, 3, TURN_CHUNKS * P], F32, name="few")
        nc.gpsimd.memset(few[:], 0.0)
        parked = out_rows[TOKENS - FRAMES : TOKENS, 0:FRAME_TABLE]

        def park_frame_tables():
            tables = few[0:FRAMES, :, 0:F_END].rearrange("p n (h d) -> p n h d", h=HEADS)
            fill_table(tables[:, 0:2, :, :], 0, angle_rows[0:FRAMES, :, 0:F_COLS], FRAMES)
            nc.sync.dma_start(out=parked.rearrange("f (n k) -> f n k", n=2), in_=few[0:FRAMES, 0:2, 0:F_END])
            nc.vector.scalar_tensor_tensor(
                out=tables[:, 2, :, :],
                in0=g_all[0:FRAMES, :].rearrange("p (h d) -> p h d", d=HEAD)[:, :, 0:F_COLS],
                scalar=-1.0,
                in1=angle_rows[0:FRAMES, 1, 0:F_COLS].unsqueeze(1).to_broadcast([FRAMES, HEADS, F_COLS]),
                op0=ALU.mult,
                op1=ALU.mult,
            )

        def fetch_frame_tables(first, last):
            nc.sync.dma_start(
                out=tab_frames[:, first:last, :, :, :].rearrange("p f n h d -> p f (n h d)"),
                in_=parked[first:last, :].unsqueeze(0).to_broadcast([P, last - first, FRAME_TABLE]),
            )

        def picked_angles(first, cols):
            return angles[:, first : first + 2 * cols].rearrange("p (n d) -> p n d", n=2)

        def fill_grid_tables(half):
            rows = (ROWS0, ROWS1)[half]
            fill_table(tab_grid[:, half, :, :, 0:GRID_COLS], F_COLS, picked_angles(rows, GRID_COLS), P)
            fill_table(tab_grid[:, half, :, :, GRID_COLS:RC_COLS], 2 * row_end, picked_angles(COLS, GRID_COLS), P)

        def fill_first_frame():
            fill_table(tab_frames[:, 0, :, :, :], 0, picked_angles(FIRST, F_COLS), P)

        turns = [const.tile([P, TURN_CHUNKS, P], F32, name="turn%d" % n) for n in range(TURN_FRAMES)]
        diagonal = const.tile([P, TURN_CHUNKS, P], F32, name="diagonal")
        turn_cols = const.tile([P, 2, TURN_CHUNKS, TURN_FRAMES], F32, name="turn_cols")
        ident_ps = {}

        def fetch_turn_columns():
            for n in range(2):
                flipped = bank_tile(X_BANKS[n], [P, TURN_CHUNKS + 1, P], "flipped")
                for q in range(TURN_CHUNKS):
                    nc.tensor.transpose(flipped[:, q, :], few[:, 2 * n, q * P : (q + 1) * P], ident[:])
                if n == 0:
                    nc.tensor.transpose(flipped[:, TURN_CHUNKS, :], ident[:], ident[:])
                    ident_ps[0] = flipped[:, TURN_CHUNKS, :]
                nc.vector.tensor_copy(
                    out=turn_cols[:, n, :, :], in_=flipped[:, 0:TURN_CHUNKS, FRAMES - TURN_FRAMES : FRAMES]
                )

        def fill_turn(f):
            for q in range(TURN_CHUNKS):
                nc.vector.tensor_scalar(
                    out=diagonal[:, q, :], in0=ident_ps[0], scalar1=turn_cols[:, 0, q, f : f + 1], scalar2=None, op0=ALU.mult
                )
            for q in range(TURN_CHUNKS):
                nc.vector.scalar_tensor_tensor(
                    out=turns[f][:, q, :].rearrange("p (j i) -> p j i", i=2),
                    in0=ident_ps[0].rearrange("p (j i) -> p j i", i=2)[:, :, ::-1],
                    scalar=turn_cols[:, 1, q, f : f + 1],
                    in1=diagonal[:, q, :].rearrange("p (j i) -> p j i", i=2),
                    op0=ALU.mult,
                    op1=ALU.add,
                )

        grouped = {}
        codes = [const.tile([P, PASSES, BLOCK], U32, name="codes%d" % blk, align_bytes=64) for blk in range(BLOCKS)]
        planes = [const.tile([P, PASSES, BLOCK], U8, name="planes%d" % blk, align_bytes=64) for blk in range(BLOCKS)]
        y_feat = {}
        warm_bank = bank_tile(3, [P, BANK], "warm_bank")

        def keep_warm(count):
            for n in range(count):
                nc.tensor.matmul(warm_bank[:], lhsT=zeros[:, 0:P], rhs=zeros[:], start=True, stop=True)

        def transpose_x(t):
            x_words = x_all[:, t, :].bitcast(F32)
            xt = bank_tile(FIRST_X_BANKS[t] if t < len(FIRST_X_BANKS) else X_BANKS[t % len(X_BANKS)], [P, PASSES, 2, P], "xt")
            for c in range(PASSES):
                for u in range(2):
                    nc.tensor.transpose(
                        xt[:, c, u, :], x_words[:, 256 * c + u : 256 * (c + 1) : 2], ident[:]
                    )
            grouped[t] = quant.tile([P, PASSES * 4 * P], BF16, name="grouped", align_bytes=64)
            copy = nc.vector.tensor_copy if t in VECTOR_X else nc.scalar.copy
            copy(
                out=grouped[t][:].bitcast(F32).rearrange("p (c r u) -> p c r u", c=PASSES, u=2),
                in_=xt[:].rearrange("p c u r -> p c r u"),
            )

        def quantise_x(t):
            blk, i = divmod(t, BLOCK_TILES)
            for c in range(PASSES):
                nc.vector.quantize_mx(
                    out=codes[blk][:, c, i * P : (i + 1) * P].bitcast(FP8X4),
                    scales=planes[blk][:, c, i * P : (i + 1) * P],
                    in_=grouped[t][:, c * 4 * P : (c + 1) * 4 * P],
                )

        def project(blk, h):
            if h == 0:
                y_feat[blk] = feat.tile([P, HEADS, BLOCK], F32, name="y_feat")
            banks = FIRST_ACC_BANKS if blk == 0 else ACC_BANKS
            acc = bank_tile(banks[h % len(banks)], [P, BLOCK], "acc")
            for c in range(PASSES):
                nc.tensor.matmul_mx(
                    out=acc[:],
                    lhsT=words[c][:, 2 * HEAD * h : 2 * HEAD * (h + 1)].bitcast(FP4X4),
                    lhsT_scale=scales[c][:, HEAD * h : HEAD * (h + 1)],
                    rhs=codes[blk][:, c, :].bitcast(FP8X4),
                    rhs_scale=planes[blk][:, c, :],
                    start=(c == 0),
                    stop=(c == PASSES - 1),
                )
            if (blk, h) in VECTOR_BIAS:
                nc.vector.tensor_scalar(
                    out=y_feat[blk][:, h, :], in0=acc[:], scalar1=b_col[:, h : h + 1], scalar2=None, op0=ALU.add
                )
            else:
                nc.scalar.activation(
                    out=y_feat[blk][:, h, :], in_=acc[:], func=ACT.Identity, bias=b_col[:, h : h + 1], scale=1.0
                )

        y_ps = {}
        sums = {}
        inv = {}

        def back(t, k):
            blk, i = divmod(t, BLOCK_TILES)
            if t < LATE_TILE:
                bank = Y_BANKS[BANKS * (t % 2) + k]
            else:
                bank = LATE_Y_BANKS[BANKS * ((t - LATE_TILE) % 3) + k]
            y_ps[t, k] = bank_tile(bank, [P, BANK_HEADS, HEAD], "y_ps")
            for hk in range(BANK_HEADS):
                nc.tensor.transpose(
                    y_ps[t, k][:, hk, :], y_feat[blk][:, k * BANK_HEADS + hk, i * P : (i + 1) * P], ident[:]
                )
            if k == 0:
                sums[t] = small.tile([P, BANKS], F32, name="sums")
            squares = work.tile([P, BANK_HEADS, HEAD], F32, name="squares%d" % k)
            nc.scalar.activation(
                out=squares[:], in_=y_ps[t, k][:], func=ACT.Square, accum_out=sums[t][:, k : k + 1]
            )

        turned = {}
        prods = {}

        def turn_back(t):
            blk, i = divmod(t, BLOCK_TILES)
            turned[t] = bank_tile(ACC_BANKS[t % len(ACC_BANKS)], [P, F_END], "turned")
            for q in range(TURN_CHUNKS):
                cols = slice(q * P, min((q + 1) * P, F_END))
                nc.tensor.matmul(
                    turned[t][:, cols], lhsT=y_feat[blk][:, q, i * P : (i + 1) * P],
                    rhs=turns[i // 2][:, q, 0 : cols.stop - cols.start], start=True, stop=True,
                )

        part = {}

        def norm_first(t):
            part[t] = small.tile([P, 1], F32, name="part")
            nc.scalar.activation(
                out=part[t][:], in_=sums[t][:, 0:1], func=ACT.Identity, bias=eps_col[:, 0:1], scale=1.0 / FEATURES
            )

        def norm(t):
            inv[t] = small.tile([P, 1], F32, name="inv")
            nc.scalar.activation(
                out=inv[t][:], in_=sums[t][:, 1:2], func=ACT.Abs_reciprocal_sqrt, bias=part[t][:, 0:1],
                scale=1.0 / FEATURES,
            )

        def rotate(t):
            frame, half = divmod(t, 2)
            prod = work.tile([P, 2, FEATURES], F32, name="prod")
            f_table = tab_frames[:, frame, :, :, :].rearrange("p n h d -> p n (h d)")
            rc_table = tab_grid[:, half, :, :, :].rearrange("p n h d -> p n (h d)")
            ranges = [
                (0, F_END, f_table),
                (F_END, BANK, rc_table[:, :, 0 : BANK - F_END]),
                (BANK, FEATURES, rc_table[:, :, BANK - F_END : FEATURES - F_END]),
            ]
            prods[t] = prod
            for first, last, table in ranges[1:] if t >= TURN_TILE else ranges:
                bank, col = divmod(first, BANK)
                pairs = y_ps[t, bank][:].rearrange("p h (j i) -> p (h j) i", i=2)[:, col // 2 : (col + last - first) // 2, :]
                for n in range(2):
                    nc.vector.scalar_tensor_tensor(
                        out=prod[:, n, first:last].rearrange("p (j i) -> p j i", i=2),
                        in0=pairs if n == 0 else pairs[:, :, ::-1],
                        scalar=inv[t][:, 0:1],
                        in1=table[:, n, :].rearrange("p (j i) -> p j i", i=2),
                        op0=ALU.mult,
                        op1=ALU.mult,
                    )
        def finish(t):
            prod = prods[t]
            rotated = outs.tile([P, HEADS, HEAD], F32, name="rotated")
            if t >= TURN_TILE:
                nc.scalar.activation(
                    out=rotated[:, :, 0:F_COLS], in_=turned[t][:].rearrange("p (h d) -> p h d", h=HEADS), func=ACT.Copy,
                    scale=inv[t][:, 0:1],
                )
            last_tile = t == TILES - 1
            count = HEADS // 2 if t >= TILES - 2 else HEADS
            for head in range(0, HEADS, count):
                for first, cols, base in FEATURE_RANGES[1:] if t >= TURN_TILE else FEATURE_RANGES:
                    cos_prod, sin_prod = [
                        prod[:, n, base + head * cols : base + (head + count) * cols].rearrange("p (h d) -> p h d", h=count)
                        for n in range(2)
                    ]
                    (nc.vector if last_tile else nc.gpsimd).tensor_tensor(
                        out=rotated[:, head : head + count, first : first + cols], in0=cos_prod, in1=sin_prod, op=ALU.add
                    )
                nc.sync.dma_start(
                    out=out_rows[t * P : (t + 1) * P, head * HEAD : (head + count) * HEAD],
                    in_=rotated[:, head : head + count, :].rearrange("p h d -> p (h d)"),
                )

        order_bias()
        keep_warm(4)
        for t in range(BLOCK_TILES):
            transpose_x(t)
            quantise_x(t)
        pick_angles()
        transpose_x(4)
        turn_bias()
        keep_warm(2)
        order_weight(0)
        project(0, 0)
        order_weight(1)
        project(0, 1)
        fill_grid_tables(0)
        project(0, 2)
        fill_first_frame()
        project(0, 3)
        quantise_x(4)
        park_frame_tables()
        fetch_frame_tables(EARLY_FRAMES, FRAMES // 2)
        fetch_frame_tables(FRAMES // 2, FRAMES - TURN_FRAMES)
        transpose_x(5)
        transpose_x(6)
        fill_grid_tables(1)
        quantise_x(5)
        quantise_x(6)
        for h in range(4, 8):
            project(0, h)
        transpose_x(7)
        quantise_x(7)
        back(0, 0)
        back(0, 1)
        for step in range(TILES):
            ahead = step + X_LEAD
            blk, i = divmod(step + MX_LEAD, BLOCK_TILES)
            if step > 0:
                back(step, 0)
                if i == 0 and ahead < TILES:
                    transpose_x(ahead)
                back(step, 1)
            norm_first(step)
            if ahead < TILES and i > 0:
                transpose_x(ahead)
            norm(step)
            if step > TURN_TILE:
                turn_back(step - 1)
                finish(step - 1)
            if step == 0:
                transpose_x(8)
                transpose_x(9)
                pass
            if blk < BLOCKS:
                for h in range(STEP_HEADS * i, STEP_HEADS * (i + 1)):
                    project(blk, h)
            rotate(step)
            if step < TURN_TILE:
                finish(step)
            if step == TILES - 1:
                turn_back(step)
                finish(step)
            if step == 7:
                fetch_turn_columns()
            if step in (8, 9):
                fill_turn(step - 8)
            if step == 0:
                quantise_x(8)
                quantise_x(9)
            elif ahead < TILES:
                quantise_x(ahead)
